import numpy as np
import ml_dtypes


def mxq(x, axis, fmt="e4m3"):
    dtype, down = {"e4m3": (ml_dtypes.float8_e4m3fn, 7), "e5m2": (ml_dtypes.float8_e5m2, 14)}[fmt]
    v = np.moveaxis(np.asarray(x, np.float32).astype(ml_dtypes.bfloat16).astype(np.float64), axis, -1)
    blocks = v.reshape(v.shape[:-1] + (-1, 32))
    amax = np.abs(blocks).max(-1, keepdims=True)
    byte = np.maximum(np.where(amax > 0, np.frexp(amax)[1] - 1 + 127, 0) - down, 1)
    scale = np.exp2(byte - 127.0)
    codes = (blocks / scale).astype(np.float32).astype(dtype).astype(np.float64)
    return np.moveaxis((codes * scale).reshape(v.shape), -1, axis)


WIDE = False


def mx_kscale(k):
    if not WIDE:
        return np.ones(k)
    levels = np.array([10, -10, 5, -5, 0])
    if k % 512:
        return np.exp2(np.random.permutation(np.resize(levels, k // 32))).repeat(32)
    a = np.empty((k // 512, 16))
    for p in range(k // 512):
        a[p, :8] = np.random.permutation(np.resize(levels, 8))
        for g in range(8):
            far = levels[np.abs(levels - a[p, g]) >= 10]
            a[p, g + 8] = far[np.random.randint(len(far))]
    return np.exp2(a.ravel()).repeat(32)


BF16 = ml_dtypes.bfloat16


def bf(x):
    return np.asarray(x, np.float32).astype(BF16)


def f64(x):
    return np.asarray(x).astype(np.float64)


B, T, P, F, G, R, C, O = 1024, 8, 768, 256, 512, 128, 4, 10


def setup_inputs():
    s, t = mx_kscale(P + F), mx_kscale(G)
    u = np.roll(t, R)
    r0 = np.concatenate([1.0 / (np.sqrt(P + F) * s), [0.1]])[:, None]
    r1 = np.concatenate([1.5 / (np.sqrt(G) * t), [0.1]])[:, None]
    return {"primary_input": bf((np.random.standard_normal((B, T, P)) * s[:P]).reshape(B, T * P)),
            "prev": bf((np.maximum(np.random.standard_normal((B, T, F)), 0.0) * 0.9 * s[P:]).reshape(B, T * F)),
            "col": bf(np.array([float(np.random.randint(1, C))])),
            "W0": bf(np.random.standard_normal((P + F + 1, G)) * r0 * u),
            "b0": bf(np.random.standard_normal(G) * 0.2 * u),
            "W1": bf(np.random.standard_normal((G + 1, F)) * r1),
            "b1": bf(np.random.standard_normal(F) * 0.2)}


def reference(primary_input, prev, col, W0, b0, W1, b1):
    w0, w1, c = f64(W0), f64(W1), f64(col)
    inp = np.concatenate([f64(primary_input).reshape(B, T, P), f64(prev).reshape(B, T, F)], axis=-1)
    a = (mxq(inp, 2, "e4m3") @ mxq(w0[:P + F], 0, "e4m3")) + c * w0[P + F] + f64(b0)
    h = np.roll(np.maximum(a, 0.0).reshape(B, T * G), -R, axis=1).reshape(B, T, G)
    y = (mxq(h, 2, "e4m3") @ mxq(w1[:G], 0, "e4m3")) + c * w1[G] + f64(b1)
    return np.roll(np.maximum(y, 0.0).reshape(B, T * F), R, axis=1)

@@ -1,0 +1,250 @@
+from contextlib import ExitStack
+
+import concourse.mybir as mybir
+from concourse.masks import make_identity
+
+F32 = mybir.dt.float32
+BF16 = mybir.dt.bfloat16
+U32 = mybir.dt.uint32
+I32 = mybir.dt.int32
+U8 = mybir.dt.uint8
+FP8X4 = mybir.dt.float8_e4m3fn_x4
+ACT = mybir.ActivationFunctionType
+ALU = mybir.AluOpType
+
+P = 128
+B, T, PK, F, G = 1024, 8, 768, 256, 512
+K = PK + F
+NCH = 2 * (B // P)
+FLOPS = 2 * B * T * (K * G + G * F)
+F32_MAX = 3.4028234663852886e38
+GPSIMD_RELU_BELOW = 14
+BR, BY = 6, 2
+
+
+def tile_capsuleneuralnetwork_pa_t_kernel(tc, primary_input, prev, col, W0, b0, W1, b1, out):
+    nc = tc.nc
+    with ExitStack() as ctx:
+        ctx.enter_context(tc.manual_schedule())
+        const = ctx.enter_context(tc.tile_pool(name="const", bufs=1))
+        xpool = ctx.enter_context(tc.tile_pool(name="xpool", bufs=8))
+        work = ctx.enter_context(tc.tile_pool(name="work", bufs=3))
+        psum = ctx.enter_context(tc.psum_pool(name="psum", bufs=1))
+
+        x_t, gx_t, xq_t, xs_t, ht_t, gh_t, hq_t, hs_t, y_t = {}, {}, {}, {}, {}, {}, {}, {}, {}
+
+        def load(k):
+            i, c = divmod(k, 2)
+            rows = slice(P * i, P * i + P)
+            x = xpool.tile([P, 4 * K], BF16, tag="x", name="x")
+            xv = x[:].rearrange("p (t k) -> p t k", t=4)
+            nc.sync.dma_start(
+                out=xv[:, :, 0:PK],
+                in_=primary_input[rows, 4 * PK * c : 4 * PK * (c + 1)].rearrange("p (t k) -> p t k", t=4),
+            )
+            nc.sync.dma_start(
+                out=xv[:, :, PK:K],
+                in_=prev[rows, 4 * F * c : 4 * F * (c + 1)].rearrange("p (t k) -> p t k", t=4),
+            )
+            x_t[k] = x
+
+        w0raw = const.tile([P, 2 * 4 * G], BF16)
+        nc.sync.dma_start(
+            out=w0raw[:].rearrange("p (g r) -> p g r", g=2),
+            in_=W0[0:K, :].rearrange("(g p j) n -> p g (j n)", g=2, j=4),
+        )
+        for k in range(5):
+            load(k)
+
+        c1 = const.tile([1, 1], BF16)
+        nc.scalar.dma_start(out=c1[:], in_=col.rearrange("(a b) -> a b", a=1))
+        wb0 = const.tile([P, G], BF16)
+        wb1 = const.tile([P, F], BF16)
+        colones = const.tile([P, P], BF16)
+        nc.vector.memset(wb0[:], 0.0)
+        nc.vector.memset(wb1[:], 0.0)
+        nc.vector.memset(colones[:], 0.0)
+        nc.vector.memset(colones[32:33, :], 1.0)
+        nc.scalar.dma_start(out=wb0[0:1, :], in_=W0[K : K + 1, :])
+        nc.scalar.dma_start(out=wb0[32:33, :], in_=b0.rearrange("(o n) -> o n", o=1))
+        nc.scalar.dma_start(out=wb1[0:1, :], in_=W1[G : G + 1, :])
+        nc.scalar.dma_start(out=wb1[32:33, :], in_=b1.rearrange("(o n) -> o n", o=1))
+        w1raw = const.tile([P, 4 * F], BF16)
+        nc.scalar.dma_start(out=w1raw[:], in_=W1[0:G, :].rearrange("(p j) f -> p (j f)", j=4))
+        nc.vector.tensor_copy(out=colones[0:1, :], in_=c1[0:1, 0:1].to_broadcast([1, P]))
+
+        ident = const.tile([P, P], F32)
+        make_identity(nc, ident[:])
+
+        w0g = const.tile([P, 2 * G * 4], BF16, align_bytes=64)
+        w0q = const.tile([P, 2 * G], U32, align_bytes=64)
+        w0s = const.tile([P, 2 * G], U8, align_bytes=64)
+        for g in range(2):
+            dst = w0g[:, 4 * G * g : 4 * G * (g + 1)].rearrange("p (s m j) -> p s m j", s=4, j=4)
+            src = w0raw[:, 4 * G * g : 4 * G * (g + 1)].rearrange("p (j m s) -> p s m j", j=4, s=4)
+            nc.vector.tensor_copy(out=dst[:, :, 0:96, :], in_=src[:, :, 32:128, :])
+            nc.vector.tensor_copy(out=dst[:, :, 96:128, :], in_=src[:, :, 0:32, :])
+        w1g = const.tile([P, F * 4], BF16, align_bytes=64)
+        w1q = const.tile([P, F], U32, align_bytes=64)
+        w1s = const.tile([P, F], U8, align_bytes=64)
+        nc.vector.tensor_copy(
+            out=w1g[:].rearrange("p (c i t) -> p c t i", i=4, t=4),
+            in_=w1raw[:].rearrange("p (t c i) -> p c t i", t=4, i=4),
+        )
+        nc.vector.quantize_mx(out=w0q[:].bitcast(FP8X4), scales=w0s[:], in_=w0g[:])
+        nc.vector.quantize_mx(out=w1q[:].bitcast(FP8X4), scales=w1s[:], in_=w1g[:])
+        wb0p = const.tile([P, G], BF16)
+        wb0d = wb0p[:].rearrange("p (s m) -> p s m", s=4)
+        wb0v = wb0[:].rearrange("p (m s) -> p s m", s=4)
+        nc.vector.tensor_copy(out=wb0d[:, :, 0:96], in_=wb0v[:, :, 32:128])
+        nc.vector.tensor_copy(out=wb0d[:, :, 96:128], in_=wb0v[:, :, 0:32])
+
+        bias1 = const.tile([P, 2 * F], F32)
+        bias0 = const.tile([P, 4], F32)
+
+        def biases():
+            pb1 = psum.tile([P, 512], F32, tag="Y", bufs=BY, name="pb1")
+            for r in range(2):
+                nc.tensor.matmul(out=pb1[:, F * r : F * (r + 1)], lhsT=colones[:], rhs=wb1[:], start=True, stop=True)
+            nc.vector.tensor_copy(out=bias1[:], in_=pb1[:])
+            pb0 = psum.tile([P, 512], F32, tag="Y", bufs=BY, name="pb0")
+            for m in range(4):
+                nc.tensor.matmul(
+                    out=pb0[:, 32 * m : 32 * (m + 1)], lhsT=wb0p[:, P * m : P * (m + 1)], rhs=colones[:, 0:32],
+                    start=True, stop=True,
+                )
+            nc.vector.tensor_copy(out=bias0[:], in_=pb0[:, 0:128].rearrange("p (m n) -> p m n", m=4)[:, :, 0])
+
+        def tr(k):
+            xw = x_t[k][:].bitcast(F32)
+            gx = work.tile([P, 4096], BF16, tag="gx", name="gx", align_bytes=64)
+            gxw = gx[:].bitcast(F32).rearrange("p (g n u) -> p g n u", g=2, u=2)
+            for g in range(2):
+                for h in range(2):
+                    tp = psum.tile([P, 512], F32, tag="R", bufs=BR, name="tp")
+                    tpv = tp[:].rearrange("p (t u b) -> p t u b", t=2, u=2)
+                    for tt in range(2):
+                        for u in range(2):
+                            w = 512 * (2 * h + tt) + 256 * g + u
+                            nc.tensor.transpose(tpv[:, tt, u, :], xw[:, w : w + 255 : 2], ident[:])
+                    nc.scalar.copy(
+                        out=gxw[:, g, 256 * h : 256 * h + 256, :].rearrange("p (t b) u -> p t b u", t=2),
+                        in_=tpv.rearrange("p t u b -> p t b u"),
+                    )
+            gx_t[k] = gx
+
+        def qx(k):
+            xq = work.tile([P, 1024], U32, tag="xq", name="xq", align_bytes=64)
+            xs = work.tile([P, 1024], U8, tag="xs", name="xs", align_bytes=64)
+            nc.vector.quantize_mx(out=xq[:].bitcast(FP8X4), scales=xs[:], in_=gx_t[k][:])
+            xq_t[k], xs_t[k] = xq, xs
+
+        def l1(k):
+            ht = work.tile([P, 2048], BF16, tag="ht", name="ht")
+            xq, xs = xq_t[k], xs_t[k]
+            for m in range(4):
+                acc = psum.tile([P, 512], F32, tag="R", bufs=BR, name="acc")
+                for g in range(2):
+                    wc = slice(G * g + P * m, G * g + P * m + P)
+                    xc = slice(512 * g, 512 * g + 512)
+                    nc.tensor.matmul_mx(
+                        out=acc[:],
+                        lhsT=w0q[:, wc].bitcast(FP8X4), lhsT_scale=w0s[:, wc],
+                        rhs=xq[:, xc].bitcast(FP8X4), rhs_scale=xs[:, xc],
+                        start=(g == 0), stop=(g == 1),
+                    )
+                nc.scalar.activation(
+                    out=ht[:, 512 * m : 512 * (m + 1)], in_=acc[:], func=ACT.Relu, bias=bias0[:, m : m + 1], scale=1.0
+                )
+            ht_t[k] = ht
+
+        def rg(k):
+            gh = work.tile([P, 2048], BF16, tag="gh", name="gh", align_bytes=64)
+            nc.vector.tensor_copy(
+                out=gh[:].rearrange("p (c i s) -> p c s i", i=4, s=4),
+                in_=ht_t[k][:].rearrange("p (s c i) -> p c s i", s=4, i=4),
+            )
+            gh_t[k] = gh
+
+        def qh(k):
+            i, c = divmod(k, 2)
+            if c == 0:
+                hq_t[i] = work.tile([P, 10 * P], U32, tag="hq", name="hq", align_bytes=64)
+                hs_t[i] = work.tile([P, 10 * P], U8, tag="hs", name="hs", align_bytes=64)
+            w = slice(640 * c, 640 * c + 512)
+            nc.vector.quantize_mx(out=hq_t[i][:, w].bitcast(FP8X4), scales=hs_t[i][:, w], in_=gh_t[k][:])
+
+        def roll(i):
+            hqw = hq_t[i][96:128, :].bitcast(I32)
+            hsw = hs_t[i][96:100, :].bitcast(I32)
+            for c in range(2):
+                for v, w in ((hqw, P), (hsw, P // 4)):
+                    nc.vector.tensor_copy(
+                        out=v[:, w * (5 * c + 4) : w * (5 * c + 5)], in_=v[:, w * 5 * (1 - c) : w * (5 * (1 - c) + 1)]
+                    )
+            for v, w in ((hqw, P), (hsw, P // 4)):
+                vv = v.rearrange("p (c n) -> p c n", c=2)
+                nc.vector.tensor_copy(out=vv[:, :, 0 : 4 * w], in_=vv[:, :, w : 5 * w])
+
+        def l2(k):
+            i, c = divmod(k, 2)
+            hq, hs = hq_t[i], hs_t[i]
+            ys = []
+            for j in range(2):
+                y = psum.tile([P, 512], F32, tag="Y", bufs=BY, name="y")
+                for tt in range(2):
+                    t0 = P * (5 * c + 2 * j + tt)
+                    hc = slice(t0, t0 + P)
+                    nc.tensor.matmul_mx(
+                        out=y[:, F * tt : F * (tt + 1)],
+                        lhsT=hq[:, hc].bitcast(FP8X4), lhsT_scale=hs[:, hc],
+                        rhs=w1q[:].bitcast(FP8X4), rhs_scale=w1s[:],
+                        start=True, stop=True,
+                    )
+                ys.append(y)
+            y_t[k] = ys
+
+        def yadd(k):
+            i, c = divmod(k, 2)
+            rows = slice(P * i, P * i + P)
+            osb = work.tile([P, 1024], F32, tag="osb", bufs=4, name="osb")
+            for j in range(2):
+                nc.vector.tensor_tensor(
+                    out=osb[:, 512 * j : 512 * (j + 1)], in0=y_t[k][j][:], in1=bias1[:], op=ALU.add
+                )
+            if k < GPSIMD_RELU_BELOW:
+                nc.gpsimd.tensor_scalar(
+                    out=osb[:], in0=osb[:], scalar1=F32_MAX, scalar2=0.0, op0=ALU.min, op1=ALU.max
+                )
+            else:
+                nc.vector.tensor_scalar_max(out=osb[:], in0=osb[:], scalar1=0.0)
+            if c == 0:
+                nc.sync.dma_start(out=out[rows, 128:1152], in_=osb[:])
+            else:
+                nc.sync.dma_start(out=out[rows, 1152:2048], in_=osb[:, 0:896])
+                nc.sync.dma_start(out=out[rows, 0:128], in_=osb[:, 896:1024])
+
+        def on(k):
+            return 0 <= k < NCH
+
+        for s in range(NCH + 5):
+            if on(s + 5):
+                load(s + 5)
+            if on(s - 2):
+                rg(s - 2)
+            if on(s):
+                tr(s)
+            if s == 0:
+                biases()
+            if on(s - 5):
+                yadd(s - 5)
+            if on(s - 1):
+                l1(s - 1)
+            if on(s - 2):
+                qh(s - 2)
+            if on(s - 4):
+                l2(s - 4)
+            if on(s):
+                qx(s)
+            if on(s - 2) and s % 2 == 1:
+                roll((s - 2) // 2)

@@ -18,7 +18,6 @@ K = PK + F
 NCH = 2 * (B // P)
 FLOPS = 2 * B * T * (K * G + G * F)
 F32_MAX = 3.4028234663852886e38
-GPSIMD_RELU_BELOW = 14
 BR, BY = 6, 2
 
 
@@ -31,7 +30,7 @@ def tile_capsuleneuralnetwork_pa_t_kernel(tc, primary_input, prev, col, W0, b0, 
         work = ctx.enter_context(tc.tile_pool(name="work", bufs=3))
         psum = ctx.enter_context(tc.psum_pool(name="psum", bufs=1))
 
-        x_t, gx_t, xq_t, xs_t, ht_t, gh_t, hq_t, hs_t, y_t = {}, {}, {}, {}, {}, {}, {}, {}, {}
+        x_t, gx_t, xq_t, xs_t, ht_t, gh_t, hq_t, hs_t, y_t, o_t = {}, {}, {}, {}, {}, {}, {}, {}, {}, {}
 
         def load(k):
             i, c = divmod(k, 2)
@@ -53,7 +52,11 @@ def tile_capsuleneuralnetwork_pa_t_kernel(tc, primary_input, prev, col, W0, b0, 
             out=w0raw[:].rearrange("p (g r) -> p g r", g=2),
             in_=W0[0:K, :].rearrange("(g p j) n -> p g (j n)", g=2, j=4),
         )
-        for k in range(5):
+        load(0)
+        load(1)
+        w1raw = const.tile([P, 4 * F], BF16)
+        nc.sync.dma_start(out=w1raw[:], in_=W1[0:G, :].rearrange("(p j) f -> p (j f)", j=4))
+        for k in range(2, 5):
             load(k)
 
         c1 = const.tile([1, 1], BF16)
@@ -69,8 +72,6 @@ def tile_capsuleneuralnetwork_pa_t_kernel(tc, primary_input, prev, col, W0, b0, 
         nc.scalar.dma_start(out=wb0[32:33, :], in_=b0.rearrange("(o n) -> o n", o=1))
         nc.scalar.dma_start(out=wb1[0:1, :], in_=W1[G : G + 1, :])
         nc.scalar.dma_start(out=wb1[32:33, :], in_=b1.rearrange("(o n) -> o n", o=1))
-        w1raw = const.tile([P, 4 * F], BF16)
-        nc.scalar.dma_start(out=w1raw[:], in_=W1[0:G, :].rearrange("(p j) f -> p (j f)", j=4))
         nc.vector.tensor_copy(out=colones[0:1, :], in_=c1[0:1, 0:1].to_broadcast([1, P]))
 
         ident = const.tile([P, P], F32)
@@ -84,15 +85,10 @@ def tile_capsuleneuralnetwork_pa_t_kernel(tc, primary_input, prev, col, W0, b0, 
             src = w0raw[:, 4 * G * g : 4 * G * (g + 1)].rearrange("p (j m s) -> p s m j", j=4, s=4)
             nc.vector.tensor_copy(out=dst[:, :, 0:96, :], in_=src[:, :, 32:128, :])
             nc.vector.tensor_copy(out=dst[:, :, 96:128, :], in_=src[:, :, 0:32, :])
+        nc.vector.quantize_mx(out=w0q[:].bitcast(FP8X4), scales=w0s[:], in_=w0g[:])
         w1g = const.tile([P, F * 4], BF16, align_bytes=64)
         w1q = const.tile([P, F], U32, align_bytes=64)
         w1s = const.tile([P, F], U8, align_bytes=64)
-        nc.vector.tensor_copy(
-            out=w1g[:].rearrange("p (c i t) -> p c t i", i=4, t=4),
-            in_=w1raw[:].rearrange("p (t c i) -> p c t i", t=4, i=4),
-        )
-        nc.vector.quantize_mx(out=w0q[:].bitcast(FP8X4), scales=w0s[:], in_=w0g[:])
-        nc.vector.quantize_mx(out=w1q[:].bitcast(FP8X4), scales=w1s[:], in_=w1g[:])
         wb0p = const.tile([P, G], BF16)
         wb0d = wb0p[:].rearrange("p (s m) -> p s m", s=4)
         wb0v = wb0[:].rearrange("p (m s) -> p s m", s=4)
@@ -101,6 +97,13 @@ def tile_capsuleneuralnetwork_pa_t_kernel(tc, primary_input, prev, col, W0, b0, 
 
         bias1 = const.tile([P, 2 * F], F32)
         bias0 = const.tile([P, 4], F32)
+
+        def weights1():
+            nc.vector.tensor_copy(
+                out=w1g[:].rearrange("p (c i t) -> p c t i", i=4, t=4),
+                in_=w1raw[:].rearrange("p (t c i) -> p c t i", t=4, i=4),
+            )
+            nc.vector.quantize_mx(out=w1q[:].bitcast(FP8X4), scales=w1s[:], in_=w1g[:])
 
         def biases():
             pb1 = psum.tile([P, 512], F32, tag="Y", bufs=BY, name="pb1")
@@ -205,19 +208,21 @@ def tile_capsuleneuralnetwork_pa_t_kernel(tc, primary_input, prev, col, W0, b0, 
             y_t[k] = ys
 
         def yadd(k):
-            i, c = divmod(k, 2)
-            rows = slice(P * i, P * i + P)
             osb = work.tile([P, 1024], F32, tag="osb", bufs=4, name="osb")
             for j in range(2):
                 nc.vector.tensor_tensor(
                     out=osb[:, 512 * j : 512 * (j + 1)], in0=y_t[k][j][:], in1=bias1[:], op=ALU.add
                 )
-            if k < GPSIMD_RELU_BELOW:
-                nc.gpsimd.tensor_scalar(
-                    out=osb[:], in0=osb[:], scalar1=F32_MAX, scalar2=0.0, op0=ALU.min, op1=ALU.max
-                )
-            else:
-                nc.vector.tensor_scalar_max(out=osb[:], in0=osb[:], scalar1=0.0)
+            nc.gpsimd.tensor_scalar(
+                out=osb[:, 0:512], in0=osb[:, 0:512], scalar1=F32_MAX, scalar2=0.0, op0=ALU.min, op1=ALU.max
+            )
+            o_t[k] = osb
+
+        def relu(k):
+            i, c = divmod(k, 2)
+            rows = slice(P * i, P * i + P)
+            osb = o_t[k]
+            nc.vector.tensor_scalar_max(out=osb[:, 512:1024], in0=osb[:, 512:1024], scalar1=0.0)
             if c == 0:
                 nc.sync.dma_start(out=out[rows, 128:1152], in_=osb[:])
             else:
@@ -230,20 +235,26 @@ def tile_capsuleneuralnetwork_pa_t_kernel(tc, primary_input, prev, col, W0, b0, 
         for s in range(NCH + 5):
             if on(s + 5):
                 load(s + 5)
-            if on(s - 2):
-                rg(s - 2)
             if on(s):
                 tr(s)
             if s == 0:
                 biases()
-            if on(s - 5):
-                yadd(s - 5)
+            if s == 1:
+                weights1()
+            if on(s - 4) and s < NCH:
+                l2(s - 4)
             if on(s - 1):
                 l1(s - 1)
+            if on(s - 4) and s >= NCH:
+                l2(s - 4)
+            if on(s - 2):
+                rg(s - 2)
+            if on(s - 5):
+                relu(s - 5)
             if on(s - 2):
                 qh(s - 2)
             if on(s - 4):
-                l2(s - 4)
+                yadd(s - 4)
             if on(s):
                 qx(s)
             if on(s - 2) and s % 2 == 1:

@@ -32,27 +32,29 @@ def tile_capsuleneuralnetwork_pa_t_kernel(tc, primary_input, prev, col, W0, b0, 
 
         x_t, gx_t, xq_t, xs_t, ht_t, gh_t, hq_t, hs_t, y_t, o_t = {}, {}, {}, {}, {}, {}, {}, {}, {}, {}
 
-        def load(k):
+        def load(k, half=None):
             i, c = divmod(k, 2)
             rows = slice(P * i, P * i + P)
-            x = xpool.tile([P, 4 * K], BF16, tag="x", name="x")
-            xv = x[:].rearrange("p (t k) -> p t k", t=4)
-            nc.sync.dma_start(
-                out=xv[:, :, 0:PK],
-                in_=primary_input[rows, 4 * PK * c : 4 * PK * (c + 1)].rearrange("p (t k) -> p t k", t=4),
-            )
-            nc.sync.dma_start(
-                out=xv[:, :, PK:K],
-                in_=prev[rows, 4 * F * c : 4 * F * (c + 1)].rearrange("p (t k) -> p t k", t=4),
-            )
-            x_t[k] = x
+            if not half:
+                x_t[k] = xpool.tile([P, 4 * K], BF16, tag="x", name="x")
+            xv = x_t[k][:].rearrange("p (t k) -> p t k", t=4)
+            pv = primary_input[rows, 4 * PK * c : 4 * PK * (c + 1)].rearrange("p (t k) -> p t k", t=4)
+            vv = prev[rows, 4 * F * c : 4 * F * (c + 1)].rearrange("p (t k) -> p t k", t=4)
+            ts = slice(0, 4) if half is None else slice(2 * half, 2 * half + 2)
+            nc.sync.dma_start(out=xv[:, ts, 0:PK], in_=pv[:, ts, :])
+            nc.sync.dma_start(out=xv[:, ts, PK:K], in_=vv[:, ts, :])
 
         w0raw = const.tile([P, 2 * 4 * G], BF16)
-        nc.sync.dma_start(
-            out=w0raw[:].rearrange("p (g r) -> p g r", g=2),
-            in_=W0[0:K, :].rearrange("(g p j) n -> p g (j n)", g=2, j=4),
-        )
-        load(0)
+        def load_w0(g):
+            nc.sync.dma_start(
+                out=w0raw[:, 4 * G * g : 4 * G * (g + 1)],
+                in_=W0[G * g : G * (g + 1), :].rearrange("(p j) n -> p (j n)", j=4),
+            )
+
+        load_w0(0)
+        load(0, 0)
+        load_w0(1)
+        load(0, 1)
         load(1)
         w1raw = const.tile([P, 4 * F], BF16)
         nc.sync.dma_start(out=w1raw[:], in_=W1[0:G, :].rearrange("(p j) f -> p (j f)", j=4))
@@ -77,6 +79,11 @@ def tile_capsuleneuralnetwork_pa_t_kernel(tc, primary_input, prev, col, W0, b0, 
         ident = const.tile([P, P], F32)
         make_identity(nc, ident[:])
 
+        wb0p = const.tile([P, G], BF16)
+        wb0d = wb0p[:].rearrange("p (s m) -> p s m", s=4)
+        wb0v = wb0[:].rearrange("p (m s) -> p s m", s=4)
+        nc.vector.tensor_copy(out=wb0d[:, :, 0:96], in_=wb0v[:, :, 32:128])
+        nc.vector.tensor_copy(out=wb0d[:, :, 96:128], in_=wb0v[:, :, 0:32])
         w0g = const.tile([P, 2 * G * 4], BF16, align_bytes=64)
         w0q = const.tile([P, 2 * G], U32, align_bytes=64)
         w0s = const.tile([P, 2 * G], U8, align_bytes=64)
@@ -85,15 +92,13 @@ def tile_capsuleneuralnetwork_pa_t_kernel(tc, primary_input, prev, col, W0, b0, 
             src = w0raw[:, 4 * G * g : 4 * G * (g + 1)].rearrange("p (j m s) -> p s m j", j=4, s=4)
             nc.vector.tensor_copy(out=dst[:, :, 0:96, :], in_=src[:, :, 32:128, :])
             nc.vector.tensor_copy(out=dst[:, :, 96:128, :], in_=src[:, :, 0:32, :])
-        nc.vector.quantize_mx(out=w0q[:].bitcast(FP8X4), scales=w0s[:], in_=w0g[:])
+            gc = slice(G * g, G * g + G)
+            nc.vector.quantize_mx(
+                out=w0q[:, gc].bitcast(FP8X4), scales=w0s[:, gc], in_=w0g[:, 4 * G * g : 4 * G * (g + 1)]
+            )
         w1g = const.tile([P, F * 4], BF16, align_bytes=64)
         w1q = const.tile([P, F], U32, align_bytes=64)
         w1s = const.tile([P, F], U8, align_bytes=64)
-        wb0p = const.tile([P, G], BF16)
-        wb0d = wb0p[:].rearrange("p (s m) -> p s m", s=4)
-        wb0v = wb0[:].rearrange("p (m s) -> p s m", s=4)
-        nc.vector.tensor_copy(out=wb0d[:, :, 0:96], in_=wb0v[:, :, 32:128])
-        nc.vector.tensor_copy(out=wb0d[:, :, 96:128], in_=wb0v[:, :, 0:32])
 
         bias1 = const.tile([P, 2 * F], F32)
         bias0 = const.tile([P, 4], F32)
@@ -105,11 +110,7 @@ def tile_capsuleneuralnetwork_pa_t_kernel(tc, primary_input, prev, col, W0, b0, 
             )
             nc.vector.quantize_mx(out=w1q[:].bitcast(FP8X4), scales=w1s[:], in_=w1g[:])
 
-        def biases():
-            pb1 = psum.tile([P, 512], F32, tag="Y", bufs=BY, name="pb1")
-            for r in range(2):
-                nc.tensor.matmul(out=pb1[:, F * r : F * (r + 1)], lhsT=colones[:], rhs=wb1[:], start=True, stop=True)
-            nc.vector.tensor_copy(out=bias1[:], in_=pb1[:])
+        def bias_of_layer_1():
             pb0 = psum.tile([P, 512], F32, tag="Y", bufs=BY, name="pb0")
             for m in range(4):
                 nc.tensor.matmul(
@@ -118,11 +119,18 @@ def tile_capsuleneuralnetwork_pa_t_kernel(tc, primary_input, prev, col, W0, b0, 
                 )
             nc.vector.tensor_copy(out=bias0[:], in_=pb0[:, 0:128].rearrange("p (m n) -> p m n", m=4)[:, :, 0])
 
-        def tr(k):
+        def bias_of_layer_2():
+            pb1 = psum.tile([P, 512], F32, tag="Y", bufs=BY, name="pb1")
+            for r in range(2):
+                nc.tensor.matmul(out=pb1[:, F * r : F * (r + 1)], lhsT=colones[:], rhs=wb1[:], start=True, stop=True)
+            nc.vector.tensor_copy(out=bias1[:], in_=pb1[:])
+
+        def tr(k, part):
             xw = x_t[k][:].bitcast(F32)
-            gx = work.tile([P, 4096], BF16, tag="gx", name="gx", align_bytes=64)
-            gxw = gx[:].bitcast(F32).rearrange("p (g n u) -> p g n u", g=2, u=2)
-            for g in range(2):
+            if part == 0:
+                gx_t[k] = work.tile([P, 4096], BF16, tag="gx", name="gx", align_bytes=64)
+            gxw = gx_t[k][:].bitcast(F32).rearrange("p (g n u) -> p g n u", g=2, u=2)
+            for g in [part]:
                 for h in range(2):
                     tp = psum.tile([P, 512], F32, tag="R", bufs=BR, name="tp")
                     tpv = tp[:].rearrange("p (t u b) -> p t u b", t=2, u=2)
@@ -134,18 +142,22 @@ def tile_capsuleneuralnetwork_pa_t_kernel(tc, primary_input, prev, col, W0, b0, 
                         out=gxw[:, g, 256 * h : 256 * h + 256, :].rearrange("p (t b) u -> p t b u", t=2),
                         in_=tpv.rearrange("p t u b -> p t b u"),
                     )
-            gx_t[k] = gx
 
-        def qx(k):
-            xq = work.tile([P, 1024], U32, tag="xq", name="xq", align_bytes=64)
-            xs = work.tile([P, 1024], U8, tag="xs", name="xs", align_bytes=64)
-            nc.vector.quantize_mx(out=xq[:].bitcast(FP8X4), scales=xs[:], in_=gx_t[k][:])
-            xq_t[k], xs_t[k] = xq, xs
+        def qx(k, g):
+            if g == 0:
+                xq_t[k] = work.tile([P, 1024], U32, tag="xq", name="xq", align_bytes=64)
+                xs_t[k] = work.tile([P, 1024], U8, tag="xs", name="xs", align_bytes=64)
+            n = slice(512 * g, 512 * g + 512)
+            nc.vector.quantize_mx(
+                out=xq_t[k][:, n].bitcast(FP8X4), scales=xs_t[k][:, n], in_=gx_t[k][:, 2048 * g : 2048 * g + 2048]
+            )
 
-        def l1(k):
-            ht = work.tile([P, 2048], BF16, tag="ht", name="ht")
+        def l1(k, part):
+            if part == 0:
+                ht_t[k] = work.tile([P, 2048], BF16, tag="ht", name="ht")
+            ht = ht_t[k]
             xq, xs = xq_t[k], xs_t[k]
-            for m in range(4):
+            for m in range(2 * part, 2 * part + 2):
                 acc = psum.tile([P, 512], F32, tag="R", bufs=BR, name="acc")
                 for g in range(2):
                     wc = slice(G * g + P * m, G * g + P * m + P)
@@ -159,7 +171,6 @@ def tile_capsuleneuralnetwork_pa_t_kernel(tc, primary_input, prev, col, W0, b0, 
                 nc.scalar.activation(
                     out=ht[:, 512 * m : 512 * (m + 1)], in_=acc[:], func=ACT.Relu, bias=bias0[:, m : m + 1], scale=1.0
                 )
-            ht_t[k] = ht
 
         def rg(k):
             gh = work.tile([P, 2048], BF16, tag="gh", name="gh", align_bytes=64)
@@ -232,30 +243,56 @@ def tile_capsuleneuralnetwork_pa_t_kernel(tc, primary_input, prev, col, W0, b0, 
         def on(k):
             return 0 <= k < NCH
 
-        for s in range(NCH + 5):
+        last = NCH - 1
+        for s in range(NCH):
             if on(s + 5):
                 load(s + 5)
-            if on(s):
-                tr(s)
-            if s == 0:
-                biases()
-            if s == 1:
-                weights1()
-            if on(s - 4) and s < NCH:
+            tr(s, 0)
+            if on(s - 1):
+                qx(s - 1, 1)
+            if on(s - 4):
                 l2(s - 4)
             if on(s - 1):
-                l1(s - 1)
-            if on(s - 4) and s >= NCH:
-                l2(s - 4)
+                l1(s - 1, 0)
+            tr(s, 1)
+            if s == 0:
+                bias_of_layer_1()
+            if on(s - 1):
+                l1(s - 1, 1)
             if on(s - 2):
                 rg(s - 2)
             if on(s - 5):
                 relu(s - 5)
+            qx(s, 0)
+            if s == 1:
+                bias_of_layer_2()
+            if s == 2:
+                weights1()
             if on(s - 2):
                 qh(s - 2)
             if on(s - 4):
                 yadd(s - 4)
-            if on(s):
-                qx(s)
+            if s == last:
+                qx(s, 1)
             if on(s - 2) and s % 2 == 1:
                 roll((s - 2) // 2)
+        l1(last, 0)
+        l1(last, 1)
+        l2(last - 3)
+        rg(last - 1)
+        relu(last - 4)
+        qh(last - 1)
+        yadd(last - 3)
+        rg(last)
+        relu(last - 3)
+        qh(last)
+        l2(last - 2)
+        yadd(last - 2)
+        roll(last // 2)
+        l2(last - 1)
+        l2(last)
+        relu(last - 2)
+        yadd(last - 1)
+        relu(last - 1)
+        yadd(last)
+        relu(last)

@@ -19,6 +19,7 @@ NCH = 2 * (B // P)
 FLOPS = 2 * B * T * (K * G + G * F)
 F32_MAX = 3.4028234663852886e38
 BR, BY = 6, 2
+ROLLED = 6
 
 
 def tile_capsuleneuralnetwork_pa_t_kernel(tc, primary_input, prev, col, W0, b0, W1, b1, out):
@@ -30,7 +31,7 @@ def tile_capsuleneuralnetwork_pa_t_kernel(tc, primary_input, prev, col, W0, b0, 
         work = ctx.enter_context(tc.tile_pool(name="work", bufs=3))
         psum = ctx.enter_context(tc.psum_pool(name="psum", bufs=1))
 
-        x_t, gx_t, xq_t, xs_t, ht_t, gh_t, hq_t, hs_t, y_t, o_t = {}, {}, {}, {}, {}, {}, {}, {}, {}, {}
+        x_t, gx_t, xq_t, xs_t, ht_t, gh_t, hq_t, hs_t, y_t, o_t, cq_t, cs_t = {}, {}, {}, {}, {}, {}, {}, {}, {}, {}, {}, {}
 
         def load(k, half=None):
             i, c = divmod(k, 2)
@@ -110,6 +111,22 @@ def tile_capsuleneuralnetwork_pa_t_kernel(tc, primary_input, prev, col, W0, b0, 
             )
             nc.vector.quantize_mx(out=w1q[:].bitcast(FP8X4), scales=w1s[:], in_=w1g[:])
 
+        w1p_t, w1q_t, w1s_t = {}, {}, {}
+
+        def weights1_parts():
+            for r in range(2):
+                w1p = const.tile([P, F * 4], BF16, name="w1p%d" % r, align_bytes=64)
+                w1q_t[r] = const.tile([P, F], U32, name="w1q%d" % r, align_bytes=64)
+                w1s_t[r] = const.tile([P, F], U8, name="w1s%d" % r, align_bytes=64)
+                own, other = (slice(0, 96), slice(96, 128)) if r == 0 else (slice(96, 128), slice(0, 96))
+                nc.gpsimd.memset(w1p[other, :], 0.0)
+                nc.gpsimd.tensor_copy(out=w1p[own, :], in_=w1g[own, :])
+                w1p_t[r] = w1p
+
+        def weights1_parts_quantised():
+            for r in range(2):
+                nc.vector.quantize_mx(out=w1q_t[r][:].bitcast(FP8X4), scales=w1s_t[r][:], in_=w1p_t[r][:])
+
         def bias_of_layer_1():
             pb0 = psum.tile([P, 512], F32, tag="Y", bufs=BY, name="pb0")
             for m in range(4):
@@ -125,12 +142,11 @@ def tile_capsuleneuralnetwork_pa_t_kernel(tc, primary_input, prev, col, W0, b0, 
                 nc.tensor.matmul(out=pb1[:, F * r : F * (r + 1)], lhsT=colones[:], rhs=wb1[:], start=True, stop=True)
             nc.vector.tensor_copy(out=bias1[:], in_=pb1[:])
 
-        def tr(k, part):
+        def tr(k):
             xw = x_t[k][:].bitcast(F32)
-            if part == 0:
-                gx_t[k] = work.tile([P, 4096], BF16, tag="gx", name="gx", align_bytes=64)
+            gx_t[k] = work.tile([P, 4096], BF16, tag="gx", name="gx", align_bytes=64)
             gxw = gx_t[k][:].bitcast(F32).rearrange("p (g n u) -> p g n u", g=2, u=2)
-            for g in [part]:
+            for g in range(2):
                 for h in range(2):
                     tp = psum.tile([P, 512], F32, tag="R", bufs=BR, name="tp")
                     tpv = tp[:].rearrange("p (t u b) -> p t u b", t=2, u=2)
@@ -143,21 +159,17 @@ def tile_capsuleneuralnetwork_pa_t_kernel(tc, primary_input, prev, col, W0, b0, 
                         in_=tpv.rearrange("p t u b -> p t b u"),
                     )
 
-        def qx(k, g):
-            if g == 0:
-                xq_t[k] = work.tile([P, 1024], U32, tag="xq", name="xq", align_bytes=64)
-                xs_t[k] = work.tile([P, 1024], U8, tag="xs", name="xs", align_bytes=64)
-            n = slice(512 * g, 512 * g + 512)
-            nc.vector.quantize_mx(
-                out=xq_t[k][:, n].bitcast(FP8X4), scales=xs_t[k][:, n], in_=gx_t[k][:, 2048 * g : 2048 * g + 2048]
-            )
+        def qx(k):
+            xq = work.tile([P, 1024], U32, tag="xq", name="xq", align_bytes=64)
+            xs = work.tile([P, 1024], U8, tag="xs", name="xs", align_bytes=64)
+            nc.vector.quantize_mx(out=xq[:].bitcast(FP8X4), scales=xs[:], in_=gx_t[k][:])
+            xq_t[k], xs_t[k] = xq, xs
 
-        def l1(k, part):
-            if part == 0:
-                ht_t[k] = work.tile([P, 2048], BF16, tag="ht", name="ht")
-            ht = ht_t[k]
+        def l1(k):
+            ht = work.tile([P, 2048], BF16, tag="ht", name="ht")
+            ht_t[k] = ht
             xq, xs = xq_t[k], xs_t[k]
-            for m in range(2 * part, 2 * part + 2):
+            for m in range(4):
                 acc = psum.tile([P, 512], F32, tag="R", bufs=BR, name="acc")
                 for g in range(2):
                     wc = slice(G * g + P * m, G * g + P * m + P)
@@ -183,22 +195,27 @@ def tile_capsuleneuralnetwork_pa_t_kernel(tc, primary_input, prev, col, W0, b0, 
         def qh(k):
             i, c = divmod(k, 2)
             if c == 0:
-                hq_t[i] = work.tile([P, 10 * P], U32, tag="hq", name="hq", align_bytes=64)
-                hs_t[i] = work.tile([P, 10 * P], U8, tag="hs", name="hs", align_bytes=64)
-            w = slice(640 * c, 640 * c + 512)
+                hq_t[i] = work.tile([P, 8 * P], U32, tag="hq", bufs=4, name="hq", align_bytes=64)
+                hs_t[i] = work.tile([P, 8 * P], U8, tag="hs", bufs=4, name="hs", align_bytes=64)
+            w = slice(512 * c, 512 * c + 512)
             nc.vector.quantize_mx(out=hq_t[i][:, w].bitcast(FP8X4), scales=hs_t[i][:, w], in_=gh_t[k][:])
 
-        def roll(i):
-            hqw = hq_t[i][96:128, :].bitcast(I32)
-            hsw = hs_t[i][96:100, :].bitcast(I32)
-            for c in range(2):
-                for v, w in ((hqw, P), (hsw, P // 4)):
-                    nc.vector.tensor_copy(
-                        out=v[:, w * (5 * c + 4) : w * (5 * c + 5)], in_=v[:, w * 5 * (1 - c) : w * (5 * (1 - c) + 1)]
-                    )
-            for v, w in ((hqw, P), (hsw, P // 4)):
-                vv = v.rearrange("p (c n) -> p c n", c=2)
-                nc.vector.tensor_copy(out=vv[:, :, 0 : 4 * w], in_=vv[:, :, w : 5 * w])
+        def roll_views(i):
+            return [
+                (t[96:rows, :].bitcast(I32), c[96:rows, :].bitcast(I32), w)
+                for t, c, rows, w in ((hq_t[i], cq_t[i], 128, P), (hs_t[i], cs_t[i], 100, P // 4))
+            ]
+
+        def roll_out(i):
+            cq_t[i] = work.tile([P, 8 * P], U32, tag="cq", name="cq")
+            cs_t[i] = work.tile([P, 8 * P], U8, tag="cs", name="cs")
+            for tv, cv, w in roll_views(i):
+                nc.sync.dma_start(out=cv, in_=tv)
+
+        def roll_back(i):
+            for tv, cv, w in roll_views(i):
+                nc.sync.dma_start(out=tv[:, 0 : 7 * w], in_=cv[:, w : 8 * w])
+                nc.sync.dma_start(out=tv[:, 7 * w : 8 * w], in_=cv[:, 0:w])
 
         def l2(k):
             i, c = divmod(k, 2)
@@ -207,14 +224,16 @@ def tile_capsuleneuralnetwork_pa_t_kernel(tc, primary_input, prev, col, W0, b0, 
             for j in range(2):
                 y = psum.tile([P, 512], F32, tag="Y", bufs=BY, name="y")
                 for tt in range(2):
-                    t0 = P * (5 * c + 2 * j + tt)
-                    hc = slice(t0, t0 + P)
-                    nc.tensor.matmul_mx(
-                        out=y[:, F * tt : F * (tt + 1)],
-                        lhsT=hq[:, hc].bitcast(FP8X4), lhsT_scale=hs[:, hc],
-                        rhs=w1q[:].bitcast(FP8X4), rhs_scale=w1s[:],
-                        start=True, stop=True,
-                    )
+                    t = 4 * c + 2 * j + tt
+                    passes = [(t, w1q, w1s)] if i < ROLLED else [(t, w1q_t[0], w1s_t[0]), ((t + 1) % T, w1q_t[1], w1s_t[1])]
+                    for n, (t, wq, ws) in enumerate(passes):
+                        hc = slice(P * t, P * t + P)
+                        nc.tensor.matmul_mx(
+                            out=y[:, F * tt : F * (tt + 1)],
+                            lhsT=hq[:, hc].bitcast(FP8X4), lhsT_scale=hs[:, hc],
+                            rhs=wq[:].bitcast(FP8X4), rhs_scale=ws[:],
+                            start=(n == 0), stop=(n == len(passes) - 1),
+                        )
                 ys.append(y)
             y_t[k] = ys
 
@@ -224,16 +243,24 @@ def tile_capsuleneuralnetwork_pa_t_kernel(tc, primary_input, prev, col, W0, b0, 
                 nc.vector.tensor_tensor(
                     out=osb[:, 512 * j : 512 * (j + 1)], in0=y_t[k][j][:], in1=bias1[:], op=ALU.add
                 )
+            o_t[k] = osb
+
+        def relu0(k):
+            osb = o_t[k]
             nc.gpsimd.tensor_scalar(
                 out=osb[:, 0:512], in0=osb[:, 0:512], scalar1=F32_MAX, scalar2=0.0, op0=ALU.min, op1=ALU.max
             )
-            o_t[k] = osb
 
-        def relu(k):
+        def relu1(k):
+            osb = o_t[k]
+            nc.gpsimd.tensor_scalar(
+                out=osb[:, 512:1024], in0=osb[:, 512:1024], scalar1=F32_MAX, scalar2=0.0, op0=ALU.min, op1=ALU.max
+            )
+
+        def store(k):
             i, c = divmod(k, 2)
             rows = slice(P * i, P * i + P)
             osb = o_t[k]
-            nc.vector.tensor_scalar_max(out=osb[:, 512:1024], in0=osb[:, 512:1024], scalar1=0.0)
             if c == 0:
                 nc.sync.dma_start(out=out[rows, 128:1152], in_=osb[:])
             else:
@@ -243,56 +270,45 @@ def tile_capsuleneuralnetwork_pa_t_kernel(tc, primary_input, prev, col, W0, b0, 
         def on(k):
             return 0 <= k < NCH
 
-        last = NCH - 1
-        for s in range(NCH):
+        def layer2_step(k):
+            return k + (5 if k // 2 < ROLLED else 4)
+
+        for s in range(NCH + 7):
+            done = [k for k in range(NCH) if layer2_step(k) == s]
             if on(s + 5):
                 load(s + 5)
-            tr(s, 0)
-            if on(s - 1):
-                qx(s - 1, 1)
-            if on(s - 4):
-                l2(s - 4)
-            if on(s - 1):
-                l1(s - 1, 0)
-            tr(s, 1)
+            if on(s):
+                tr(s)
             if s == 0:
                 bias_of_layer_1()
+            if s < NCH:
+                for k in done:
+                    l2(k)
             if on(s - 1):
-                l1(s - 1, 1)
+                l1(s - 1)
+            if s >= NCH:
+                for k in done:
+                    l2(k)
             if on(s - 2):
                 rg(s - 2)
-            if on(s - 5):
-                relu(s - 5)
-            qx(s, 0)
+            for k in done:
+                yadd(k)
+                relu0(k)
+                relu1(k)
+            if on(s - 2):
+                qh(s - 2)
+            if on(s):
+                qx(s)
             if s == 1:
                 bias_of_layer_2()
             if s == 2:
                 weights1()
-            if on(s - 2):
-                qh(s - 2)
-            if on(s - 4):
-                yadd(s - 4)
-            if s == last:
-                qx(s, 1)
-            if on(s - 2) and s % 2 == 1:
-                roll((s - 2) // 2)
-        l1(last, 0)
-        l1(last, 1)
-        l2(last - 3)
-        rg(last - 1)
-        relu(last - 4)
-        qh(last - 1)
-        yadd(last - 3)
-        rg(last)
-        relu(last - 3)
-        qh(last)
-        l2(last - 2)
-        yadd(last - 2)
-        roll(last // 2)
-        l2(last - 1)
-        l2(last)
-        relu(last - 2)
-        yadd(last - 1)
-        relu(last - 1)
-        yadd(last)
-        relu(last)
+                weights1_parts()
+            if s == 3:
+                weights1_parts_quantised()
+            if s % 2 == 1 and on(s - 2) and (s - 2) // 2 < ROLLED:
+                roll_out((s - 2) // 2)
+            if s % 2 == 1 and on(s - 2) and (s - 2) // 2 < ROLLED:
+                roll_back((s - 2) // 2)
+            for k in done:
+                store(k)

@@ -19,7 +19,7 @@ NCH = 2 * (B // P)
 FLOPS = 2 * B * T * (K * G + G * F)
 F32_MAX = 3.4028234663852886e38
 BR, BY = 6, 2
-ROLLED = 6
+ROLLED = 5
 
 
 def tile_capsuleneuralnetwork_pa_t_kernel(tc, primary_input, prev, col, W0, b0, W1, b1, out):
@@ -31,7 +31,7 @@ def tile_capsuleneuralnetwork_pa_t_kernel(tc, primary_input, prev, col, W0, b0, 
         work = ctx.enter_context(tc.tile_pool(name="work", bufs=3))
         psum = ctx.enter_context(tc.psum_pool(name="psum", bufs=1))
 
-        x_t, gx_t, xq_t, xs_t, ht_t, gh_t, hq_t, hs_t, y_t, o_t, cq_t, cs_t = {}, {}, {}, {}, {}, {}, {}, {}, {}, {}, {}, {}
+        x_t, gx_t, xq_t, xs_t, ht_t, gh_t, hq_t, hs_t, y_t, o_t, cq_t, cs_t, pm_t = {}, {}, {}, {}, {}, {}, {}, {}, {}, {}, {}, {}, {}
 
         def load(k, half=None):
             i, c = divmod(k, 2)
@@ -142,18 +142,30 @@ def tile_capsuleneuralnetwork_pa_t_kernel(tc, primary_input, prev, col, W0, b0, 
                 nc.tensor.matmul(out=pb1[:, F * r : F * (r + 1)], lhsT=colones[:], rhs=wb1[:], start=True, stop=True)
             nc.vector.tensor_copy(out=bias1[:], in_=pb1[:])
 
-        def tr(k):
+        def perm(k):
+            pm_t[k] = work.tile([P, 256 * 2], F32, tag="pm", bufs=3, name="pm")
+            nc.vector.tensor_copy(
+                out=pm_t[k][:].rearrange("p (t u w) -> p t u w", t=2, u=2),
+                in_=x_t[k][:].bitcast(F32).rearrange("p (t g w u) -> p g t u w", t=4, g=2, u=2)[:, 0, 0:2, :, :],
+            )
+
+        def tr(k, g0, g1):
             xw = x_t[k][:].bitcast(F32)
-            gx_t[k] = work.tile([P, 4096], BF16, tag="gx", name="gx", align_bytes=64)
+            permuted = k in pm_t
+            if permuted:
+                pm = pm_t[k][:].rearrange("p (t u w) -> p t u w", t=2, u=2)
+            if g0 == 0:
+                gx_t[k] = work.tile([P, 4096], BF16, tag="gx", name="gx", align_bytes=64)
             gxw = gx_t[k][:].bitcast(F32).rearrange("p (g n u) -> p g n u", g=2, u=2)
-            for g in range(2):
+            for g in range(g0, g1):
                 for h in range(2):
                     tp = psum.tile([P, 512], F32, tag="R", bufs=BR, name="tp")
                     tpv = tp[:].rearrange("p (t u b) -> p t u b", t=2, u=2)
                     for tt in range(2):
                         for u in range(2):
                             w = 512 * (2 * h + tt) + 256 * g + u
-                            nc.tensor.transpose(tpv[:, tt, u, :], xw[:, w : w + 255 : 2], ident[:])
+                            words = pm[:, tt, u, :] if permuted and g == 0 and h == 0 else xw[:, w : w + 255 : 2]
+                            nc.tensor.transpose(tpv[:, tt, u, :], words, ident[:])
                     nc.scalar.copy(
                         out=gxw[:, g, 256 * h : 256 * h + 256, :].rearrange("p (t b) u -> p t b u", t=2),
                         in_=tpv.rearrange("p t u b -> p t b u"),
@@ -165,11 +177,12 @@ def tile_capsuleneuralnetwork_pa_t_kernel(tc, primary_input, prev, col, W0, b0, 
             nc.vector.quantize_mx(out=xq[:].bitcast(FP8X4), scales=xs[:], in_=gx_t[k][:])
             xq_t[k], xs_t[k] = xq, xs
 
-        def l1(k):
-            ht = work.tile([P, 2048], BF16, tag="ht", name="ht")
-            ht_t[k] = ht
+        def l1(k, m0, m1):
+            if m0 == 0:
+                ht_t[k] = work.tile([P, 2048], BF16, tag="ht", name="ht")
+            ht = ht_t[k]
             xq, xs = xq_t[k], xs_t[k]
-            for m in range(4):
+            for m in range(m0, m1):
                 acc = psum.tile([P, 512], F32, tag="R", bufs=BR, name="acc")
                 for g in range(2):
                     wc = slice(G * g + P * m, G * g + P * m + P)
@@ -270,45 +283,77 @@ def tile_capsuleneuralnetwork_pa_t_kernel(tc, primary_input, prev, col, W0, b0, 
         def on(k):
             return 0 <= k < NCH
 
-        def layer2_step(k):
-            return k + (5 if k // 2 < ROLLED else 4)
+        def layer1_step(k):
+            return k + 1 if k < 1 else k + 2
 
-        for s in range(NCH + 7):
+        def regroup_step(k):
+            return layer1_step(k) + 1
+
+        def layer2_step(k):
+            return regroup_step(k | 1) + (2 + k % 2 if k // 2 < ROLLED else 1)
+
+        for s in range(NCH):
+            layer1 = [k for k in range(NCH) if layer1_step(k) == s]
+            regroup = [k for k in range(NCH) if regroup_step(k) == s]
             done = [k for k in range(NCH) if layer2_step(k) == s]
             if on(s + 5):
                 load(s + 5)
-            if on(s):
-                tr(s)
+            tr(s, 0, 2)
             if s == 0:
                 bias_of_layer_1()
-            if s < NCH:
-                for k in done:
-                    l2(k)
-            if on(s - 1):
-                l1(s - 1)
-            if s >= NCH:
-                for k in done:
-                    l2(k)
-            if on(s - 2):
-                rg(s - 2)
+            for k in done:
+                l2(k)
+            for k in layer1:
+                l1(k, 0, 4)
+            for k in regroup:
+                rg(k)
             for k in done:
                 yadd(k)
                 relu0(k)
                 relu1(k)
-            if on(s - 2):
-                qh(s - 2)
-            if on(s):
-                qx(s)
+            for k in regroup:
+                qh(k)
+            qx(s)
+            if 3 <= s + 2 < NCH:
+                perm(s + 2)
             if s == 1:
                 bias_of_layer_2()
-            if s == 2:
+            if s == 3:
                 weights1()
                 weights1_parts()
-            if s == 3:
+            if s == 5:
                 weights1_parts_quantised()
-            if s % 2 == 1 and on(s - 2) and (s - 2) // 2 < ROLLED:
-                roll_out((s - 2) // 2)
-            if s % 2 == 1 and on(s - 2) and (s - 2) // 2 < ROLLED:
-                roll_back((s - 2) // 2)
+            for k in regroup:
+                if k % 2 == 1 and k // 2 < ROLLED:
+                    roll_out(k // 2)
+                    roll_back(k // 2)
             for k in done:
                 store(k)
+        l1(14, 0, 4)
+        l1(15, 0, 4)
+        rg(13)
+        qh(13)
+        rg(14)
+        l2(12)
+        yadd(12)
+        relu0(12)
+        relu1(12)
+        store(12)
+        qh(14)
+        rg(15)
+        l2(13)
+        yadd(13)
+        relu0(13)
+        relu1(13)
+        store(13)
+        qh(15)
+        l2(14)
+        yadd(14)
+        relu0(14)
+        relu1(14)
+        store(14)
+        l2(15)
+        yadd(15)
+        relu0(15)
+        relu1(15)
+        store(15)

@@ -19,7 +19,7 @@ NCH = 2 * (B // P)
 FLOPS = 2 * B * T * (K * G + G * F)
 F32_MAX = 3.4028234663852886e38
 BR, BY = 6, 2
-ROLLED = 5
+ROLLED = 6
 
 
 def tile_capsuleneuralnetwork_pa_t_kernel(tc, primary_input, prev, col, W0, b0, W1, b1, out):
@@ -143,17 +143,17 @@ def tile_capsuleneuralnetwork_pa_t_kernel(tc, primary_input, prev, col, W0, b0, 
             nc.vector.tensor_copy(out=bias1[:], in_=pb1[:])
 
         def perm(k):
-            pm_t[k] = work.tile([P, 256 * 2], F32, tag="pm", bufs=3, name="pm")
+            pm_t[k] = work.tile([P, 256 * 4], F32, tag="pm", bufs=3, name="pm")
             nc.vector.tensor_copy(
-                out=pm_t[k][:].rearrange("p (t u w) -> p t u w", t=2, u=2),
-                in_=x_t[k][:].bitcast(F32).rearrange("p (t g w u) -> p g t u w", t=4, g=2, u=2)[:, 0, 0:2, :, :],
+                out=pm_t[k][:].rearrange("p (t u w) -> p t u w", t=4, u=2),
+                in_=x_t[k][:].bitcast(F32).rearrange("p (t g w u) -> p g t u w", t=4, g=2, u=2)[:, 0, :, :, :],
             )
 
         def tr(k, g0, g1):
             xw = x_t[k][:].bitcast(F32)
             permuted = k in pm_t
             if permuted:
-                pm = pm_t[k][:].rearrange("p (t u w) -> p t u w", t=2, u=2)
+                pm = pm_t[k][:].rearrange("p (t u w) -> p t u w", t=4, u=2)
             if g0 == 0:
                 gx_t[k] = work.tile([P, 4096], BF16, tag="gx", name="gx", align_bytes=64)
             gxw = gx_t[k][:].bitcast(F32).rearrange("p (g n u) -> p g n u", g=2, u=2)
@@ -164,7 +164,7 @@ def tile_capsuleneuralnetwork_pa_t_kernel(tc, primary_input, prev, col, W0, b0, 
                     for tt in range(2):
                         for u in range(2):
                             w = 512 * (2 * h + tt) + 256 * g + u
-                            words = pm[:, tt, u, :] if permuted and g == 0 and h == 0 else xw[:, w : w + 255 : 2]
+                            words = pm[:, 2 * h + tt, u, :] if permuted and g == 0 else xw[:, w : w + 255 : 2]
                             nc.tensor.transpose(tpv[:, tt, u, :], words, ident[:])
                     nc.scalar.copy(
                         out=gxw[:, g, 256 * h : 256 * h + 256, :].rearrange("p (t b) u -> p t b u", t=2),
@@ -182,20 +182,25 @@ def tile_capsuleneuralnetwork_pa_t_kernel(tc, primary_input, prev, col, W0, b0, 
                 ht_t[k] = work.tile([P, 2048], BF16, tag="ht", name="ht")
             ht = ht_t[k]
             xq, xs = xq_t[k], xs_t[k]
-            for m in range(m0, m1):
-                acc = psum.tile([P, 512], F32, tag="R", bufs=BR, name="acc")
+            for h in range(m0 // 2, m1 // 2):
+                accs = {}
                 for g in range(2):
-                    wc = slice(G * g + P * m, G * g + P * m + P)
-                    xc = slice(512 * g, 512 * g + 512)
-                    nc.tensor.matmul_mx(
-                        out=acc[:],
-                        lhsT=w0q[:, wc].bitcast(FP8X4), lhsT_scale=w0s[:, wc],
-                        rhs=xq[:, xc].bitcast(FP8X4), rhs_scale=xs[:, xc],
-                        start=(g == 0), stop=(g == 1),
+                    for m in (2 * h, 2 * h + 1):
+                        if g == 0:
+                            accs[m] = psum.tile([P, 512], F32, tag="R", bufs=BR, name="acc")
+                        wc = slice(G * g + P * m, G * g + P * m + P)
+                        xc = slice(512 * g, 512 * g + 512)
+                        nc.tensor.matmul_mx(
+                            out=accs[m][:],
+                            lhsT=w0q[:, wc].bitcast(FP8X4), lhsT_scale=w0s[:, wc],
+                            rhs=xq[:, xc].bitcast(FP8X4), rhs_scale=xs[:, xc],
+                            start=(g == 0), stop=(g == 1),
+                        )
+                for m in (2 * h, 2 * h + 1):
+                    nc.scalar.activation(
+                        out=ht[:, 512 * m : 512 * (m + 1)], in_=accs[m][:], func=ACT.Relu,
+                        bias=bias0[:, m : m + 1], scale=1.0,
                     )
-                nc.scalar.activation(
-                    out=ht[:, 512 * m : 512 * (m + 1)], in_=acc[:], func=ACT.Relu, bias=bias0[:, m : m + 1], scale=1.0
-                )
 
         def rg(k):
             gh = work.tile([P, 2048], BF16, tag="gh", name="gh", align_bytes=64)
@@ -259,16 +264,22 @@ def tile_capsuleneuralnetwork_pa_t_kernel(tc, primary_input, prev, col, W0, b0, 
             o_t[k] = osb
 
         def relu0(k):
-            osb = o_t[k]
-            nc.gpsimd.tensor_scalar(
-                out=osb[:, 0:512], in0=osb[:, 0:512], scalar1=F32_MAX, scalar2=0.0, op0=ALU.min, op1=ALU.max
-            )
+            half = o_t[k][:, 0:512]
+            if k < 12:
+                nc.gpsimd.tensor_scalar(
+                    out=half, in0=half, scalar1=F32_MAX, scalar2=0.0, op0=ALU.min, op1=ALU.max
+                )
+            else:
+                nc.scalar.activation(out=half, in_=half, func=ACT.Relu)
 
         def relu1(k):
-            osb = o_t[k]
-            nc.gpsimd.tensor_scalar(
-                out=osb[:, 512:1024], in0=osb[:, 512:1024], scalar1=F32_MAX, scalar2=0.0, op0=ALU.min, op1=ALU.max
-            )
+            half = o_t[k][:, 512:1024]
+            if k < 12:
+                nc.gpsimd.tensor_scalar(
+                    out=half, in0=half, scalar1=F32_MAX, scalar2=0.0, op0=ALU.min, op1=ALU.max
+                )
+            else:
+                nc.scalar.activation(out=half, in_=half, func=ACT.Relu)
 
         def store(k):
             i, c = divmod(k, 2)
@@ -292,19 +303,20 @@ def tile_capsuleneuralnetwork_pa_t_kernel(tc, primary_input, prev, col, W0, b0, 
         def layer2_step(k):
             return regroup_step(k | 1) + (2 + k % 2 if k // 2 < ROLLED else 1)
 
-        for s in range(NCH):
+        for s in range(NCH + 5):
             layer1 = [k for k in range(NCH) if layer1_step(k) == s]
             regroup = [k for k in range(NCH) if regroup_step(k) == s]
             done = [k for k in range(NCH) if layer2_step(k) == s]
             if on(s + 5):
                 load(s + 5)
-            tr(s, 0, 2)
+            if on(s):
+                tr(s, 0, 2)
             if s == 0:
                 bias_of_layer_1()
-            for k in done:
-                l2(k)
             for k in layer1:
                 l1(k, 0, 4)
+            for k in done:
+                l2(k)
             for k in regroup:
                 rg(k)
             for k in done:
@@ -313,7 +325,8 @@ def tile_capsuleneuralnetwork_pa_t_kernel(tc, primary_input, prev, col, W0, b0, 
                 relu1(k)
             for k in regroup:
                 qh(k)
-            qx(s)
+            if on(s):
+                qx(s)
             if 3 <= s + 2 < NCH:
                 perm(s + 2)
             if s == 1:
@@ -329,31 +342,3 @@ def tile_capsuleneuralnetwork_pa_t_kernel(tc, primary_input, prev, col, W0, b0, 
                     roll_back(k // 2)
             for k in done:
                 store(k)
-        l1(14, 0, 4)
-        l1(15, 0, 4)
-        rg(13)
-        qh(13)
-        rg(14)
-        l2(12)
-        yadd(12)
-        relu0(12)
-        relu1(12)
-        store(12)
-        qh(14)
-        rg(15)
-        l2(13)
-        yadd(13)
-        relu0(13)
-        relu1(13)
-        store(13)
-        qh(15)
-        l2(14)
-        yadd(14)
-        relu0(14)
-        relu1(14)
-        store(14)
-        l2(15)
-        yadd(15)
-        relu0(15)
-        relu1(15)
-        store(15)

@@ -31,19 +31,17 @@ def tile_capsuleneuralnetwork_pa_t_kernel(tc, primary_input, prev, col, W0, b0, 
         work = ctx.enter_context(tc.tile_pool(name="work", bufs=3))
         psum = ctx.enter_context(tc.psum_pool(name="psum", bufs=1))
 
-        x_t, gx_t, xq_t, xs_t, ht_t, gh_t, hq_t, hs_t, y_t, o_t, cq_t, cs_t, pm_t = {}, {}, {}, {}, {}, {}, {}, {}, {}, {}, {}, {}, {}
+        xp_t, xv_t, gx_t, xq_t, xs_t, ht_t, gh_t, hq_t, hs_t, y_t, o_t, cq_t, cs_t, pm_t = {}, {}, {}, {}, {}, {}, {}, {}, {}, {}, {}, {}, {}, {}
 
         def load(k, half=None):
             i, c = divmod(k, 2)
             rows = slice(P * i, P * i + P)
             if not half:
-                x_t[k] = xpool.tile([P, 4 * K], BF16, tag="x", name="x")
-            xv = x_t[k][:].rearrange("p (t k) -> p t k", t=4)
-            pv = primary_input[rows, 4 * PK * c : 4 * PK * (c + 1)].rearrange("p (t k) -> p t k", t=4)
-            vv = prev[rows, 4 * F * c : 4 * F * (c + 1)].rearrange("p (t k) -> p t k", t=4)
-            ts = slice(0, 4) if half is None else slice(2 * half, 2 * half + 2)
-            nc.sync.dma_start(out=xv[:, ts, 0:PK], in_=pv[:, ts, :])
-            nc.sync.dma_start(out=xv[:, ts, PK:K], in_=vv[:, ts, :])
+                xp_t[k] = xpool.tile([P, 4 * PK], BF16, tag="xp", name="xp")
+                xv_t[k] = xpool.tile([P, 4 * F], BF16, tag="xv", name="xv")
+            lo, hi = (0, 4) if half is None else (2 * half, 2 * half + 2)
+            for tile, src, n in ((xp_t[k], primary_input, PK), (xv_t[k], prev, F)):
+                nc.sync.dma_start(out=tile[:, n * lo : n * hi], in_=src[rows, n * (4 * c + lo) : n * (4 * c + hi)])
 
         w0raw = const.tile([P, 2 * 4 * G], BF16)
         def load_w0(g):
@@ -143,17 +141,17 @@ def tile_capsuleneuralnetwork_pa_t_kernel(tc, primary_input, prev, col, W0, b0, 
             nc.vector.tensor_copy(out=bias1[:], in_=pb1[:])
 
         def perm(k):
-            pm_t[k] = work.tile([P, 256 * 4], F32, tag="pm", bufs=3, name="pm")
-            nc.vector.tensor_copy(
-                out=pm_t[k][:].rearrange("p (t u w) -> p t u w", t=4, u=2),
-                in_=x_t[k][:].bitcast(F32).rearrange("p (t g w u) -> p g t u w", t=4, g=2, u=2)[:, 0, :, :, :],
-            )
+            copy = nc.scalar.copy if k < 2 else nc.vector.tensor_copy
+            pm_t[k] = work.tile([P, 1024], F32, tag="pm", bufs=3, name="pm")
+            pv = pm_t[k][:].rearrange("p (t u w) -> p t u w", t=4, u=2)
+            xp = xp_t[k][:].bitcast(F32).rearrange("p (t g w u) -> p g t u w", t=4, g=3, u=2)
+            xv = xv_t[k][:].bitcast(F32).rearrange("p (t w u) -> p t u w", t=4, u=2)
+            copy(out=pv[:, :, :, 0:64], in_=xp[:, 2, :, :, :])
+            copy(out=pv[:, :, :, 64:128], in_=xv)
 
         def tr(k, g0, g1):
-            xw = x_t[k][:].bitcast(F32)
-            permuted = k in pm_t
-            if permuted:
-                pm = pm_t[k][:].rearrange("p (t u w) -> p t u w", t=4, u=2)
+            xw = xp_t[k][:].bitcast(F32)
+            pm = pm_t[k][:].rearrange("p (t u w) -> p t u w", t=4, u=2)
             if g0 == 0:
                 gx_t[k] = work.tile([P, 4096], BF16, tag="gx", name="gx", align_bytes=64)
             gxw = gx_t[k][:].bitcast(F32).rearrange("p (g n u) -> p g n u", g=2, u=2)
@@ -163,8 +161,8 @@ def tile_capsuleneuralnetwork_pa_t_kernel(tc, primary_input, prev, col, W0, b0, 
                     tpv = tp[:].rearrange("p (t u b) -> p t u b", t=2, u=2)
                     for tt in range(2):
                         for u in range(2):
-                            w = 512 * (2 * h + tt) + 256 * g + u
-                            words = pm[:, 2 * h + tt, u, :] if permuted and g == 0 else xw[:, w : w + 255 : 2]
+                            w = 384 * (2 * h + tt) + u
+                            words = xw[:, w : w + 255 : 2] if g == 0 else pm[:, 2 * h + tt, u, :]
                             nc.tensor.transpose(tpv[:, tt, u, :], words, ident[:])
                     nc.scalar.copy(
                         out=gxw[:, g, 256 * h : 256 * h + 256, :].rearrange("p (t b) u -> p t b u", t=2),
@@ -309,6 +307,8 @@ def tile_capsuleneuralnetwork_pa_t_kernel(tc, primary_input, prev, col, W0, b0, 
             done = [k for k in range(NCH) if layer2_step(k) == s]
             if on(s + 5):
                 load(s + 5)
+            if s < 2:
+                perm(s)
             if on(s):
                 tr(s, 0, 2)
             if s == 0:
@@ -327,7 +327,7 @@ def tile_capsuleneuralnetwork_pa_t_kernel(tc, primary_input, prev, col, W0, b0, 
                 qh(k)
             if on(s):
                 qx(s)
-            if 3 <= s + 2 < NCH:
+            if on(s + 2):
                 perm(s + 2)
             if s == 1:
                 bias_of_layer_2()

@@ -19,6 +19,7 @@ NCH = 2 * (B // P)
 FLOPS = 2 * B * T * (K * G + G * F)
 F32_MAX = 3.4028234663852886e38
 BR, BY = 6, 2
+JOINED = 2
 ROLLED = 6
 
 
@@ -27,21 +28,28 @@ def tile_capsuleneuralnetwork_pa_t_kernel(tc, primary_input, prev, col, W0, b0, 
     with ExitStack() as ctx:
         ctx.enter_context(tc.manual_schedule())
         const = ctx.enter_context(tc.tile_pool(name="const", bufs=1))
-        xpool = ctx.enter_context(tc.tile_pool(name="xpool", bufs=8))
+        xpool = ctx.enter_context(tc.tile_pool(name="xpool", bufs=7))
         work = ctx.enter_context(tc.tile_pool(name="work", bufs=3))
         psum = ctx.enter_context(tc.psum_pool(name="psum", bufs=1))
 
-        xp_t, xv_t, gx_t, xq_t, xs_t, ht_t, gh_t, hq_t, hs_t, y_t, o_t, cq_t, cs_t, pm_t = {}, {}, {}, {}, {}, {}, {}, {}, {}, {}, {}, {}, {}, {}
+        x_t, xp_t, xv_t, gx_t, xq_t, xs_t, ht_t, gh_t, hq_t, hs_t, y_t, o_t, cq_t, cs_t, pm_t = {}, {}, {}, {}, {}, {}, {}, {}, {}, {}, {}, {}, {}, {}, {}
 
-        def load(k, half=None):
+        def load(k, lo=0, hi=4):
             i, c = divmod(k, 2)
             rows = slice(P * i, P * i + P)
-            if not half:
+            p_in = primary_input[rows, PK * (4 * c + lo) : PK * (4 * c + hi)]
+            v_in = prev[rows, F * (4 * c + lo) : F * (4 * c + hi)]
+            if k < JOINED:
+                if lo == 0:
+                    x_t[k] = xpool.tile([P, 4 * K], BF16, tag="x", bufs=JOINED, name="x")
+                x = x_t[k][:, K * lo : K * hi].rearrange("p (t k) -> p t k", k=K)
+                nc.sync.dma_start(out=x[:, :, 0:PK], in_=p_in.rearrange("p (t k) -> p t k", k=PK))
+                nc.sync.dma_start(out=x[:, :, PK:K], in_=v_in.rearrange("p (t k) -> p t k", k=F))
+            else:
                 xp_t[k] = xpool.tile([P, 4 * PK], BF16, tag="xp", name="xp")
+                nc.sync.dma_start(out=xp_t[k][:], in_=p_in)
                 xv_t[k] = xpool.tile([P, 4 * F], BF16, tag="xv", name="xv")
-            lo, hi = (0, 4) if half is None else (2 * half, 2 * half + 2)
-            for tile, src, n in ((xp_t[k], primary_input, PK), (xv_t[k], prev, F)):
-                nc.sync.dma_start(out=tile[:, n * lo : n * hi], in_=src[rows, n * (4 * c + lo) : n * (4 * c + hi)])
+                nc.sync.dma_start(out=xv_t[k][:], in_=v_in)
 
         w0raw = const.tile([P, 2 * 4 * G], BF16)
         def load_w0(g):
@@ -51,9 +59,9 @@ def tile_capsuleneuralnetwork_pa_t_kernel(tc, primary_input, prev, col, W0, b0, 
             )
 
         load_w0(0)
-        load(0, 0)
+        load(0, 0, 2)
         load_w0(1)
-        load(0, 1)
+        load(0, 2, 4)
         load(1)
         w1raw = const.tile([P, 4 * F], BF16)
         nc.sync.dma_start(out=w1raw[:], in_=W1[0:G, :].rearrange("(p j) f -> p (j f)", j=4))
@@ -141,17 +149,24 @@ def tile_capsuleneuralnetwork_pa_t_kernel(tc, primary_input, prev, col, W0, b0, 
             nc.vector.tensor_copy(out=bias1[:], in_=pb1[:])
 
         def perm(k):
-            copy = nc.scalar.copy if k < 2 else nc.vector.tensor_copy
             pm_t[k] = work.tile([P, 1024], F32, tag="pm", bufs=3, name="pm")
             pv = pm_t[k][:].rearrange("p (t u w) -> p t u w", t=4, u=2)
             xp = xp_t[k][:].bitcast(F32).rearrange("p (t g w u) -> p g t u w", t=4, g=3, u=2)
             xv = xv_t[k][:].bitcast(F32).rearrange("p (t w u) -> p t u w", t=4, u=2)
-            copy(out=pv[:, :, :, 0:64], in_=xp[:, 2, :, :, :])
-            copy(out=pv[:, :, :, 64:128], in_=xv)
+            nc.vector.tensor_copy(out=pv[:, :, :, 0:64], in_=xp[:, 2, :, :, :])
+            nc.vector.tensor_copy(out=pv[:, :, :, 64:128], in_=xv)
+
+        def words(k, t, g, u):
+            if k < JOINED:
+                w = 512 * t + 256 * g + u
+                return x_t[k][:].bitcast(F32)[:, w : w + 255 : 2]
+            if g == 1:
+                w = 256 * t + 128 * u
+                return pm_t[k][:, w : w + 128]
+            w = 384 * t + u
+            return xp_t[k][:].bitcast(F32)[:, w : w + 255 : 2]
 
         def tr(k, g0, g1):
-            xw = xp_t[k][:].bitcast(F32)
-            pm = pm_t[k][:].rearrange("p (t u w) -> p t u w", t=4, u=2)
             if g0 == 0:
                 gx_t[k] = work.tile([P, 4096], BF16, tag="gx", name="gx", align_bytes=64)
             gxw = gx_t[k][:].bitcast(F32).rearrange("p (g n u) -> p g n u", g=2, u=2)
@@ -161,9 +176,7 @@ def tile_capsuleneuralnetwork_pa_t_kernel(tc, primary_input, prev, col, W0, b0, 
                     tpv = tp[:].rearrange("p (t u b) -> p t u b", t=2, u=2)
                     for tt in range(2):
                         for u in range(2):
-                            w = 384 * (2 * h + tt) + u
-                            words = xw[:, w : w + 255 : 2] if g == 0 else pm[:, 2 * h + tt, u, :]
-                            nc.tensor.transpose(tpv[:, tt, u, :], words, ident[:])
+                            nc.tensor.transpose(tpv[:, tt, u, :], words(k, 2 * h + tt, g, u), ident[:])
                     nc.scalar.copy(
                         out=gxw[:, g, 256 * h : 256 * h + 256, :].rearrange("p (t b) u -> p t b u", t=2),
                         in_=tpv.rearrange("p t u b -> p t b u"),
@@ -201,12 +214,13 @@ def tile_capsuleneuralnetwork_pa_t_kernel(tc, primary_input, prev, col, W0, b0, 
                     )
 
         def rg(k):
-            gh = work.tile([P, 2048], BF16, tag="gh", name="gh", align_bytes=64)
-            nc.vector.tensor_copy(
-                out=gh[:].rearrange("p (c i s) -> p c s i", i=4, s=4),
-                in_=ht_t[k][:].rearrange("p (s c i) -> p c s i", s=4, i=4),
-            )
-            gh_t[k] = gh
+            gh_t[k] = work.tile([P, 2048], BF16, tag="gh", name="gh", align_bytes=64)
+            dst = gh_t[k][:].rearrange("p (c i s) -> p c s i", i=4, s=4)
+            src = ht_t[k][:].rearrange("p (s c i) -> p c s i", s=4, i=4)
+            n = P if k < 14 else 88
+            nc.vector.tensor_copy(out=dst[:, 0:n], in_=src[:, 0:n])
+            if n < P:
+                nc.scalar.copy(out=dst[:, n:P], in_=src[:, n:P])
 
         def qh(k):
             i, c = divmod(k, 2)
@@ -238,7 +252,8 @@ def tile_capsuleneuralnetwork_pa_t_kernel(tc, primary_input, prev, col, W0, b0, 
             hq, hs = hq_t[i], hs_t[i]
             ys = []
             for j in range(2):
-                y = psum.tile([P, 512], F32, tag="Y", bufs=BY, name="y")
+                tag, bufs = ("Y", BY) if k < 11 else ("R", BR)
+                y = psum.tile([P, 512], F32, tag=tag, bufs=bufs, name="y")
                 for tt in range(2):
                     t = 4 * c + 2 * j + tt
                     passes = [(t, w1q, w1s)] if i < ROLLED else [(t, w1q_t[0], w1s_t[0]), ((t + 1) % T, w1q_t[1], w1s_t[1])]
@@ -279,15 +294,21 @@ def tile_capsuleneuralnetwork_pa_t_kernel(tc, primary_input, prev, col, W0, b0, 
             else:
                 nc.scalar.activation(out=half, in_=half, func=ACT.Relu)
 
-        def store(k):
+        def store(k, lo=0, hi=1024):
             i, c = divmod(k, 2)
             rows = slice(P * i, P * i + P)
-            osb = o_t[k]
-            if c == 0:
-                nc.sync.dma_start(out=out[rows, 128:1152], in_=osb[:])
-            else:
-                nc.sync.dma_start(out=out[rows, 1152:2048], in_=osb[:, 0:896])
-                nc.sync.dma_start(out=out[rows, 0:128], in_=osb[:, 896:1024])
+            at = P + 1024 * c
+            n = min(hi, T * F - at)
+            nc.sync.dma_start(out=out[rows, at + lo : at + n], in_=o_t[k][:, lo:n])
+            if n < hi:
+                nc.sync.dma_start(out=out[rows, 0 : hi - n], in_=o_t[k][:, n:hi])
+
+        def add(k):
+            yadd(k)
+            relu0(k)
+            store(k, 0, 512)
+            relu1(k)
+            store(k, 512, 1024)
 
         def on(k):
             return 0 <= k < NCH
@@ -301,14 +322,18 @@ def tile_capsuleneuralnetwork_pa_t_kernel(tc, primary_input, prev, col, W0, b0, 
         def layer2_step(k):
             return regroup_step(k | 1) + (2 + k % 2 if k // 2 < ROLLED else 1)
 
-        for s in range(NCH + 5):
+        for s in range(NCH + 1):
             layer1 = [k for k in range(NCH) if layer1_step(k) == s]
             regroup = [k for k in range(NCH) if regroup_step(k) == s]
+            quantised = [k for k in range(NCH) if (k if k in (0, NCH - 1) else k + 1) == s]
+            before = [k for k in range(NCH) if layer2_step(k) + 1 == s <= NCH]
             done = [k for k in range(NCH) if layer2_step(k) == s]
+            for k in before:
+                yadd(k)
+                relu0(k)
+                relu1(k)
             if on(s + 5):
                 load(s + 5)
-            if s < 2:
-                perm(s)
             if on(s):
                 tr(s, 0, 2)
             if s == 0:
@@ -319,15 +344,16 @@ def tile_capsuleneuralnetwork_pa_t_kernel(tc, primary_input, prev, col, W0, b0, 
                 l2(k)
             for k in regroup:
                 rg(k)
-            for k in done:
-                yadd(k)
-                relu0(k)
-                relu1(k)
+            if s >= NCH:
+                for k in done:
+                    yadd(k)
+                    relu0(k)
+                    relu1(k)
+            for k in quantised:
+                qx(k)
             for k in regroup:
                 qh(k)
-            if on(s):
-                qx(s)
-            if on(s + 2):
+            if JOINED <= s + 2 < NCH:
                 perm(s + 2)
             if s == 1:
                 bias_of_layer_2()
@@ -340,5 +366,17 @@ def tile_capsuleneuralnetwork_pa_t_kernel(tc, primary_input, prev, col, W0, b0, 
                 if k % 2 == 1 and k // 2 < ROLLED:
                     roll_out(k // 2)
                     roll_back(k // 2)
-            for k in done:
+            for k in before + (done if s >= NCH else []):
                 store(k)
+        l2(11)
+        l1(15, 0, 4)
+        rg(14)
+        add(11)
+        qh(14)
+        rg(15)
+        l2(12)
+        add(12)
+        qh(15)
+        for k in (13, 14, 15):
+            l2(k)
+            add(k)

from contextlib import ExitStack

import concourse.mybir as mybir
from concourse.masks import make_identity

F32 = mybir.dt.float32
BF16 = mybir.dt.bfloat16
U32 = mybir.dt.uint32
I32 = mybir.dt.int32
U8 = mybir.dt.uint8
FP8X4 = mybir.dt.float8_e4m3fn_x4
ACT = mybir.ActivationFunctionType
ALU = mybir.AluOpType

P = 128
B, T, PK, F, G = 1024, 8, 768, 256, 512
K = PK + F
NCH = 2 * (B // P)
FLOPS = 2 * B * T * (K * G + G * F)
F32_MAX = 3.4028234663852886e38
BR, BY = 6, 2
JOINED = 2
ROLLED = 6


def tile_capsuleneuralnetwork_pa_t_kernel(tc, primary_input, prev, col, W0, b0, W1, b1, out):
    nc = tc.nc
    with ExitStack() as ctx:
        ctx.enter_context(tc.manual_schedule())
        const = ctx.enter_context(tc.tile_pool(name="const", bufs=1))
        xpool = ctx.enter_context(tc.tile_pool(name="xpool", bufs=7))
        work = ctx.enter_context(tc.tile_pool(name="work", bufs=3))
        psum = ctx.enter_context(tc.psum_pool(name="psum", bufs=1))

        x_t, xp_t, xv_t, gx_t, xq_t, xs_t, ht_t, gh_t, hq_t, hs_t, y_t, o_t, cq_t, cs_t, pm_t = {}, {}, {}, {}, {}, {}, {}, {}, {}, {}, {}, {}, {}, {}, {}

        def load(k, lo=0, hi=4):
            i, c = divmod(k, 2)
            rows = slice(P * i, P * i + P)
            p_in = primary_input[rows, PK * (4 * c + lo) : PK * (4 * c + hi)]
            v_in = prev[rows, F * (4 * c + lo) : F * (4 * c + hi)]
            if k < JOINED:
                if lo == 0:
                    x_t[k] = xpool.tile([P, 4 * K], BF16, tag="x", bufs=JOINED, name="x")
                x = x_t[k][:, K * lo : K * hi].rearrange("p (t k) -> p t k", k=K)
                nc.sync.dma_start(out=x[:, :, 0:PK], in_=p_in.rearrange("p (t k) -> p t k", k=PK))
                nc.sync.dma_start(out=x[:, :, PK:K], in_=v_in.rearrange("p (t k) -> p t k", k=F))
            else:
                xp_t[k] = xpool.tile([P, 4 * PK], BF16, tag="xp", name="xp")
                nc.sync.dma_start(out=xp_t[k][:], in_=p_in)
                xv_t[k] = xpool.tile([P, 4 * F], BF16, tag="xv", name="xv")
                nc.sync.dma_start(out=xv_t[k][:], in_=v_in)

        w0raw = const.tile([P, 2 * 4 * G], BF16)
        def load_w0(g):
            nc.sync.dma_start(
                out=w0raw[:, 4 * G * g : 4 * G * (g + 1)],
                in_=W0[G * g : G * (g + 1), :].rearrange("(p j) n -> p (j n)", j=4),
            )

        load_w0(0)
        load(0, 0, 2)
        load_w0(1)
        load(0, 2, 4)
        load(1)
        w1raw = const.tile([P, 4 * F], BF16)
        nc.sync.dma_start(out=w1raw[:], in_=W1[0:G, :].rearrange("(p j) f -> p (j f)", j=4))
        for k in range(2, 5):
            load(k)

        c1 = const.tile([1, 1], BF16)
        nc.scalar.dma_start(out=c1[:], in_=col.rearrange("(a b) -> a b", a=1))
        wb0 = const.tile([P, G], BF16)
        wb1 = const.tile([P, F], BF16)
        colones = const.tile([P, P], BF16)
        nc.vector.memset(wb0[:], 0.0)
        nc.vector.memset(wb1[:], 0.0)
        nc.vector.memset(colones[:], 0.0)
        nc.vector.memset(colones[32:33, :], 1.0)
        nc.scalar.dma_start(out=wb0[0:1, :], in_=W0[K : K + 1, :])
        nc.scalar.dma_start(out=wb0[32:33, :], in_=b0.rearrange("(o n) -> o n", o=1))
        nc.scalar.dma_start(out=wb1[0:1, :], in_=W1[G : G + 1, :])
        nc.scalar.dma_start(out=wb1[32:33, :], in_=b1.rearrange("(o n) -> o n", o=1))
        nc.vector.tensor_copy(out=colones[0:1, :], in_=c1[0:1, 0:1].to_broadcast([1, P]))

        ident = const.tile([P, P], F32)
        make_identity(nc, ident[:])

        wb0p = const.tile([P, G], BF16)
        wb0d = wb0p[:].rearrange("p (s m) -> p s m", s=4)
        wb0v = wb0[:].rearrange("p (m s) -> p s m", s=4)
        nc.vector.tensor_copy(out=wb0d[:, :, 0:96], in_=wb0v[:, :, 32:128])
        nc.vector.tensor_copy(out=wb0d[:, :, 96:128], in_=wb0v[:, :, 0:32])
        w0g = const.tile([P, 2 * G * 4], BF16, align_bytes=64)
        w0q = const.tile([P, 2 * G], U32, align_bytes=64)
        w0s = const.tile([P, 2 * G], U8, align_bytes=64)
        for g in range(2):
            dst = w0g[:, 4 * G * g : 4 * G * (g + 1)].rearrange("p (s m j) -> p s m j", s=4, j=4)
            src = w0raw[:, 4 * G * g : 4 * G * (g + 1)].rearrange("p (j m s) -> p s m j", j=4, s=4)
            nc.vector.tensor_copy(out=dst[:, :, 0:96, :], in_=src[:, :, 32:128, :])
            nc.vector.tensor_copy(out=dst[:, :, 96:128, :], in_=src[:, :, 0:32, :])
            gc = slice(G * g, G * g + G)
            nc.vector.quantize_mx(
                out=w0q[:, gc].bitcast(FP8X4), scales=w0s[:, gc], in_=w0g[:, 4 * G * g : 4 * G * (g + 1)]
            )
        w1g = const.tile([P, F * 4], BF16, align_bytes=64)
        w1q = const.tile([P, F], U32, align_bytes=64)
        w1s = const.tile([P, F], U8, align_bytes=64)

        bias1 = const.tile([P, 2 * F], F32)
        bias0 = const.tile([P, 4], F32)

        def weights1():
            nc.vector.tensor_copy(
                out=w1g[:].rearrange("p (c i t) -> p c t i", i=4, t=4),
                in_=w1raw[:].rearrange("p (t c i) -> p c t i", t=4, i=4),
            )
            nc.vector.quantize_mx(out=w1q[:].bitcast(FP8X4), scales=w1s[:], in_=w1g[:])

        w1p_t, w1q_t, w1s_t = {}, {}, {}

        def weights1_parts():
            for r in range(2):
                w1p = const.tile([P, F * 4], BF16, name="w1p%d" % r, align_bytes=64)
                w1q_t[r] = const.tile([P, F], U32, name="w1q%d" % r, align_bytes=64)
                w1s_t[r] = const.tile([P, F], U8, name="w1s%d" % r, align_bytes=64)
                own, other = (slice(0, 96), slice(96, 128)) if r == 0 else (slice(96, 128), slice(0, 96))
                nc.gpsimd.memset(w1p[other, :], 0.0)
                nc.gpsimd.tensor_copy(out=w1p[own, :], in_=w1g[own, :])
                w1p_t[r] = w1p

        def weights1_parts_quantised():
            for r in range(2):
                nc.vector.quantize_mx(out=w1q_t[r][:].bitcast(FP8X4), scales=w1s_t[r][:], in_=w1p_t[r][:])

        def bias_of_layer_1():
            pb0 = psum.tile([P, 512], F32, tag="Y", bufs=BY, name="pb0")
            for m in range(4):
                nc.tensor.matmul(
                    out=pb0[:, 32 * m : 32 * (m + 1)], lhsT=wb0p[:, P * m : P * (m + 1)], rhs=colones[:, 0:32],
                    start=True, stop=True,
                )
            nc.vector.tensor_copy(out=bias0[:], in_=pb0[:, 0:128].rearrange("p (m n) -> p m n", m=4)[:, :, 0])

        def bias_of_layer_2():
            pb1 = psum.tile([P, 512], F32, tag="Y", bufs=BY, name="pb1")
            for r in range(2):
                nc.tensor.matmul(out=pb1[:, F * r : F * (r + 1)], lhsT=colones[:], rhs=wb1[:], start=True, stop=True)
            nc.vector.tensor_copy(out=bias1[:], in_=pb1[:])

        def perm(k):
            pm_t[k] = work.tile([P, 1024], F32, tag="pm", bufs=3, name="pm")
            pv = pm_t[k][:].rearrange("p (t u w) -> p t u w", t=4, u=2)
            xp = xp_t[k][:].bitcast(F32).rearrange("p (t g w u) -> p g t u w", t=4, g=3, u=2)
            xv = xv_t[k][:].bitcast(F32).rearrange("p (t w u) -> p t u w", t=4, u=2)
            nc.vector.tensor_copy(out=pv[:, :, :, 0:64], in_=xp[:, 2, :, :, :])
            nc.vector.tensor_copy(out=pv[:, :, :, 64:128], in_=xv)

        def words(k, t, g, u):
            if k < JOINED:
                w = 512 * t + 256 * g + u
                return x_t[k][:].bitcast(F32)[:, w : w + 255 : 2]
            if g == 1:
                w = 256 * t + 128 * u
                return pm_t[k][:, w : w + 128]
            w = 384 * t + u
            return xp_t[k][:].bitcast(F32)[:, w : w + 255 : 2]

        def tr(k, g0, g1):
            if g0 == 0:
                gx_t[k] = work.tile([P, 4096], BF16, tag="gx", name="gx", align_bytes=64)
            gxw = gx_t[k][:].bitcast(F32).rearrange("p (g n u) -> p g n u", g=2, u=2)
            for g in range(g0, g1):
                for h in range(2):
                    tp = psum.tile([P, 512], F32, tag="R", bufs=BR, name="tp")
                    tpv = tp[:].rearrange("p (t u b) -> p t u b", t=2, u=2)
                    for tt in range(2):
                        for u in range(2):
                            nc.tensor.transpose(tpv[:, tt, u, :], words(k, 2 * h + tt, g, u), ident[:])
                    nc.scalar.copy(
                        out=gxw[:, g, 256 * h : 256 * h + 256, :].rearrange("p (t b) u -> p t b u", t=2),
                        in_=tpv.rearrange("p t u b -> p t b u"),
                    )

        def qx(k):
            xq = work.tile([P, 1024], U32, tag="xq", name="xq", align_bytes=64)
            xs = work.tile([P, 1024], U8, tag="xs", name="xs", align_bytes=64)
            nc.vector.quantize_mx(out=xq[:].bitcast(FP8X4), scales=xs[:], in_=gx_t[k][:])
            xq_t[k], xs_t[k] = xq, xs

        def l1(k, m0, m1):
            if m0 == 0:
                ht_t[k] = work.tile([P, 2048], BF16, tag="ht", name="ht")
            ht = ht_t[k]
            xq, xs = xq_t[k], xs_t[k]
            for h in range(m0 // 2, m1 // 2):
                accs = {}
                for g in range(2):
                    for m in (2 * h, 2 * h + 1):
                        if g == 0:
                            accs[m] = psum.tile([P, 512], F32, tag="R", bufs=BR, name="acc")
                        wc = slice(G * g + P * m, G * g + P * m + P)
                        xc = slice(512 * g, 512 * g + 512)
                        nc.tensor.matmul_mx(
                            out=accs[m][:],
                            lhsT=w0q[:, wc].bitcast(FP8X4), lhsT_scale=w0s[:, wc],
                            rhs=xq[:, xc].bitcast(FP8X4), rhs_scale=xs[:, xc],
                            start=(g == 0), stop=(g == 1),
                        )
                for m in (2 * h, 2 * h + 1):
                    nc.scalar.activation(
                        out=ht[:, 512 * m : 512 * (m + 1)], in_=accs[m][:], func=ACT.Relu,
                        bias=bias0[:, m : m + 1], scale=1.0,
                    )

        def rg(k):
            gh_t[k] = work.tile([P, 2048], BF16, tag="gh", name="gh", align_bytes=64)
            dst = gh_t[k][:].rearrange("p (c i s) -> p c s i", i=4, s=4)
            src = ht_t[k][:].rearrange("p (s c i) -> p c s i", s=4, i=4)
            n = P if k < 14 else 88
            nc.vector.tensor_copy(out=dst[:, 0:n], in_=src[:, 0:n])
            if n < P:
                nc.scalar.copy(out=dst[:, n:P], in_=src[:, n:P])

        def qh(k):
            i, c = divmod(k, 2)
            if c == 0:
                hq_t[i] = work.tile([P, 8 * P], U32, tag="hq", bufs=4, name="hq", align_bytes=64)
                hs_t[i] = work.tile([P, 8 * P], U8, tag="hs", bufs=4, name="hs", align_bytes=64)
            w = slice(512 * c, 512 * c + 512)
            nc.vector.quantize_mx(out=hq_t[i][:, w].bitcast(FP8X4), scales=hs_t[i][:, w], in_=gh_t[k][:])

        def roll_views(i):
            return [
                (t[96:rows, :].bitcast(I32), c[96:rows, :].bitcast(I32), w)
                for t, c, rows, w in ((hq_t[i], cq_t[i], 128, P), (hs_t[i], cs_t[i], 100, P // 4))
            ]

        def roll_out(i):
            cq_t[i] = work.tile([P, 8 * P], U32, tag="cq", name="cq")
            cs_t[i] = work.tile([P, 8 * P], U8, tag="cs", name="cs")
            for tv, cv, w in roll_views(i):
                nc.sync.dma_start(out=cv, in_=tv)

        def roll_back(i):
            for tv, cv, w in roll_views(i):
                nc.sync.dma_start(out=tv[:, 0 : 7 * w], in_=cv[:, w : 8 * w])
                nc.sync.dma_start(out=tv[:, 7 * w : 8 * w], in_=cv[:, 0:w])

        def l2(k):
            i, c = divmod(k, 2)
            hq, hs = hq_t[i], hs_t[i]
            ys = []
            for j in range(2):
                tag, bufs = ("Y", BY) if k < 11 else ("R", BR)
                y = psum.tile([P, 512], F32, tag=tag, bufs=bufs, name="y")
                for tt in range(2):
                    t = 4 * c + 2 * j + tt
                    passes = [(t, w1q, w1s)] if i < ROLLED else [(t, w1q_t[0], w1s_t[0]), ((t + 1) % T, w1q_t[1], w1s_t[1])]
                    for n, (t, wq, ws) in enumerate(passes):
                        hc = slice(P * t, P * t + P)
                        nc.tensor.matmul_mx(
                            out=y[:, F * tt : F * (tt + 1)],
                            lhsT=hq[:, hc].bitcast(FP8X4), lhsT_scale=hs[:, hc],
                            rhs=wq[:].bitcast(FP8X4), rhs_scale=ws[:],
                            start=(n == 0), stop=(n == len(passes) - 1),
                        )
                ys.append(y)
            y_t[k] = ys

        def yadd(k):
            osb = work.tile([P, 1024], F32, tag="osb", bufs=4, name="osb")
            for j in range(2):
                nc.vector.tensor_tensor(
                    out=osb[:, 512 * j : 512 * (j + 1)], in0=y_t[k][j][:], in1=bias1[:], op=ALU.add
                )
            o_t[k] = osb

        def relu0(k):
            half = o_t[k][:, 0:512]
            if k < 12:
                nc.gpsimd.tensor_scalar(
                    out=half, in0=half, scalar1=F32_MAX, scalar2=0.0, op0=ALU.min, op1=ALU.max
                )
            else:
                nc.scalar.activation(out=half, in_=half, func=ACT.Relu)

        def relu1(k):
            half = o_t[k][:, 512:1024]
            if k < 12:
                nc.gpsimd.tensor_scalar(
                    out=half, in0=half, scalar1=F32_MAX, scalar2=0.0, op0=ALU.min, op1=ALU.max
                )
            else:
                nc.scalar.activation(out=half, in_=half, func=ACT.Relu)

        def store(k, lo=0, hi=1024):
            i, c = divmod(k, 2)
            rows = slice(P * i, P * i + P)
            at = P + 1024 * c
            n = min(hi, T * F - at)
            nc.sync.dma_start(out=out[rows, at + lo : at + n], in_=o_t[k][:, lo:n])
            if n < hi:
                nc.sync.dma_start(out=out[rows, 0 : hi - n], in_=o_t[k][:, n:hi])

        def add(k):
            yadd(k)
            relu0(k)
            store(k, 0, 512)
            relu1(k)
            store(k, 512, 1024)

        def on(k):
            return 0 <= k < NCH

        def layer1_step(k):
            return k + 1 if k < 1 else k + 2

        def regroup_step(k):
            return layer1_step(k) + 1

        def layer2_step(k):
            return regroup_step(k | 1) + (2 + k % 2 if k // 2 < ROLLED else 1)

        for s in range(NCH + 1):
            layer1 = [k for k in range(NCH) if layer1_step(k) == s]
            regroup = [k for k in range(NCH) if regroup_step(k) == s]
            quantised = [k for k in range(NCH) if (k if k in (0, NCH - 1) else k + 1) == s]
            before = [k for k in range(NCH) if layer2_step(k) + 1 == s <= NCH]
            done = [k for k in range(NCH) if layer2_step(k) == s]
            for k in before:
                yadd(k)
                relu0(k)
                relu1(k)
            if on(s + 5):
                load(s + 5)
            if on(s):
                tr(s, 0, 2)
            if s == 0:
                bias_of_layer_1()
            for k in layer1:
                l1(k, 0, 4)
            for k in done:
                l2(k)
            for k in regroup:
                rg(k)
            if s >= NCH:
                for k in done:
                    yadd(k)
                    relu0(k)
                    relu1(k)
            for k in quantised:
                qx(k)
            for k in regroup:
                qh(k)
            if JOINED <= s + 2 < NCH:
                perm(s + 2)
            if s == 1:
                bias_of_layer_2()
            if s == 3:
                weights1()
                weights1_parts()
            if s == 5:
                weights1_parts_quantised()
            for k in regroup:
                if k % 2 == 1 and k // 2 < ROLLED:
                    roll_out(k // 2)
                    roll_back(k // 2)
            for k in before + (done if s >= NCH else []):
                store(k)
        l2(11)
        l1(15, 0, 4)
        rg(14)
        add(11)
        qh(14)
        rg(15)
        l2(12)
        add(12)
        qh(15)
        for k in (13, 14, 15):
            l2(k)
            add(k)
